import numpy as np
import ml_dtypes


def mxq(x, axis, fmt="e4m3"):
    dtype, down = {"e4m3": (ml_dtypes.float8_e4m3fn, 7), "e5m2": (ml_dtypes.float8_e5m2, 14)}[fmt]
    v = np.moveaxis(np.asarray(x, np.float32).astype(ml_dtypes.bfloat16).astype(np.float64), axis, -1)
    blocks = v.reshape(v.shape[:-1] + (-1, 32))
    amax = np.abs(blocks).max(-1, keepdims=True)
    byte = np.maximum(np.where(amax > 0, np.frexp(amax)[1] - 1 + 127, 0) - down, 1)
    scale = np.exp2(byte - 127.0)
    codes = (blocks / scale).astype(np.float32).astype(dtype).astype(np.float64)
    return np.moveaxis((codes * scale).reshape(v.shape), -1, axis)


WIDE = False


def mx_kscale(k):
    if not WIDE:
        return np.ones(k)
    levels = np.array([10, -10, 5, -5, 0])
    if k % 512:
        return np.exp2(np.random.permutation(np.resize(levels, k // 32))).repeat(32)
    a = np.empty((k // 512, 16))
    for p in range(k // 512):
        a[p, :8] = np.random.permutation(np.resize(levels, 8))
        for g in range(8):
            far = levels[np.abs(levels - a[p, g]) >= 10]
            a[p, g + 8] = far[np.random.randint(len(far))]
    return np.exp2(a.ravel()).repeat(32)


BF16 = ml_dtypes.bfloat16


def bf(x):
    return np.asarray(x, np.float32).astype(BF16)


def f64(x):
    return np.asarray(x).astype(np.float64)


B, H, N, D = 2, 2, 1024, 512
LOG100 = np.log(100.0)


def unit(x):
    return x / np.sqrt((x * x).sum(-1, keepdims=True))


def setup_inputs():
    logit_scale = LOG100 + np.linspace(-3.0, 1.0, H) + 0.1 * np.random.standard_normal(H)
    soft = np.exp(np.minimum(logit_scale, LOG100)) / np.sqrt(D) < 1.8
    t = np.where(soft[:, None], mx_kscale(N)[None, :], 1.0)
    return {"q_hat": bf(unit(np.random.standard_normal((B, H, N, D)))),
            "k_hat": bf(unit(np.random.standard_normal((B, H, N, D)))),
            "v": bf(np.random.standard_normal((B, H, N, D)) * (t.mean(1, keepdims=True) / t)[None, :, :, None]),
            "logit_scale": bf(logit_scale.reshape(H, 1, 1)),
            "bias": bf(np.random.standard_normal((H, N, N)) + np.log(t)[:, None, :])}


def reference(q_hat, k_hat, v, logit_scale, bias):
    scores = f64(q_hat) @ f64(k_hat).transpose(0, 1, 3, 2)
    scale = np.exp(np.minimum(f64(logit_scale), LOG100))
    scores = scores * scale[None] + f64(bias)[None]
    e = np.exp(scores - scores.max(-1, keepdims=True))
    x = (mxq(e, 3, "e4m3") @ mxq(f64(v), 2, "e4m3")) / e.sum(-1, keepdims=True)
    return x.transpose(0, 2, 1, 3).reshape(B, -1, N * D)

@@ -1,0 +1,313 @@
+from contextlib import ExitStack
+
+import concourse.mybir as mybir
+from concourse.masks import make_identity
+
+F32 = mybir.dt.float32
+BF16 = mybir.dt.bfloat16
+U32 = mybir.dt.uint32
+U8 = mybir.dt.uint8
+FP8X4 = mybir.dt.float8_e4m3fn_x4
+ALU = mybir.AluOpType
+ACT = mybir.ActivationFunctionType
+AXIS = mybir.AxisListType
+
+WINDOWS, NHEADS, N, D = 2, 2, 1024, 512
+P = 128
+TILES = N // P
+BANK = 512
+PACK = 4
+PASSES = N // (P * PACK)
+HEADS = [(0, 0), (1, 0), (0, 1), (1, 1)]
+ALL_TILES = len(HEADS) * TILES
+FLOPS = 2 * 2 * WINDOWS * NHEADS * N * N * D
+
+EXP_LAG = 1
+TRANSPOSE_LAG = 2
+QUANTISE_LAG = 3
+MX_LAG = 4
+
+UNITS_BEFORE_A_HEAD = (0, 1, 4, 2, 3)
+UNITS_IN_A_HEAD = (5, 6, 7)
+
+V_PIECES = 8
+V_PIECES_A_STEP = 2
+V_FIRST_STEP = 3
+
+
+def tile_attention_pa_t_kernel(tc, q_hat, k_hat, v, logit_scale, bias, out):
+    nc = tc.nc
+    q_rows = q_hat.rearrange("b h n d -> (b h n) d")
+    k_rows = k_hat.rearrange("b h n d -> (b h n) d")
+    v_rows = v.rearrange("b h n d -> (b h n) d")
+    bias_rows = bias.rearrange("h q k -> (h q) k")
+    out_rows = out.rearrange("b x (n h d) -> (b x n) h d", h=NHEADS, d=D)
+
+    with ExitStack() as ctx:
+        const = ctx.enter_context(tc.tile_pool(name="const", bufs=1))
+        raw = ctx.enter_context(tc.tile_pool(name="raw", bufs=2))
+        operands = ctx.enter_context(tc.tile_pool(name="operands", bufs=2))
+        work = ctx.enter_context(tc.tile_pool(name="work", bufs=4))
+        columns = ctx.enter_context(tc.tile_pool(name="columns", bufs=8))
+        score_banks = ctx.enter_context(tc.psum_pool(name="score_banks", bufs=4))
+        transpose_banks = ctx.enter_context(tc.psum_pool(name="transpose_banks", bufs=3))
+        output_banks = ctx.enter_context(tc.psum_pool(name="output_banks", bufs=1))
+        ctx.enter_context(tc.manual_schedule())
+
+        q_raw, k_raw, v_raw, q_t, k_t, v_grouped, v_words, v_scales, unit_bank = {}, {}, {}, {}, {}, {}, {}, {}, {}
+        score, neg_s, neg_max, row_sum, inv_sum, e_bf, e_bank, e_grouped, e_words, e_scales, x_bank = (
+            {}, {}, {}, {}, {}, {}, {}, {}, {}, {}, {},
+        )
+
+        def first_row(head):
+            b, h = HEADS[head]
+            return (b * NHEADS + h) * N
+
+        def load_keys(dst, rows, row0, first, count):
+            nc.sync.dma_start(
+                out=dst[:, first : first + count, :].rearrange("p (g t) d -> p g t d", t=PACK),
+                in_=rows[row0 + first * P : row0 + (first + count) * P, :].rearrange(
+                    "(g p t) d -> p g t d", p=P, t=PACK
+                ),
+            )
+
+        def load_blocks(dst, rows, row0, first, count):
+            nc.sync.dma_start(
+                out=dst[:, first : first + count, :],
+                in_=rows[row0 + first * P : row0 + (first + count) * P, :].rearrange("(t p) d -> p t d", p=P),
+            )
+
+        def new_head(head):
+            q_raw[head] = raw.tile([P, TILES, D], BF16, name="q_raw")
+            k_raw[head] = raw.tile([P, TILES, D], BF16, name="k_raw")
+            v_raw[head] = raw.tile([P, TILES, D], BF16, name="v_raw")
+            q_t[head] = operands.tile([P, TILES, 2, P], F32, name="q_t")
+            k_t[head] = operands.tile([P, 2, N], F32, name="k_t")
+
+        def unit_transposes(head, unit):
+            bank = transpose_banks.tile([P, 4, P], F32, name="unit_bank", tag="bank")
+            unit_bank[(head, unit)] = bank
+            for m in range(4):
+                if unit < 4:
+                    key_half, u = divmod(unit, 2)
+                    src = k_raw[head][:, 4 * key_half + m, 2 * u * P : 2 * (u + 1) * P]
+                else:
+                    tile_in_pair, u = divmod(m, 2)
+                    src = q_raw[head][:, 2 * (unit - 4) + tile_in_pair, 2 * u * P : 2 * (u + 1) * P]
+                nc.tensor.transpose(bank[:, m, :], src.bitcast(F32), identity_f32[:])
+
+        def unit_copy(head, unit, on_vector):
+            if unit < 4:
+                key_half, u = divmod(unit, 2)
+                dst = k_t[head][:, u, key_half * BANK : (key_half + 1) * BANK]
+            else:
+                dst = q_t[head][:, 2 * (unit - 4) : 2 * (unit - 3), :, :].rearrange("p i u q -> p (i u q)")
+            src = unit_bank[(head, unit)][:].rearrange("p m c -> p (m c)")
+            if on_vector:
+                nc.vector.tensor_copy(out=dst, in_=src)
+            else:
+                nc.scalar.copy(out=dst, in_=src)
+
+        def regroup_v(head, piece):
+            if piece == 0:
+                v_grouped[head] = operands.tile([P, PASSES, D, PACK], BF16, name="v_grouped", bufs=1, align_bytes=64)
+            g, part = divmod(piece, V_PIECES // PASSES)
+            width = D * PASSES // V_PIECES
+            nc.gpsimd.tensor_scalar(
+                out=v_grouped[head][:, g, part * width : (part + 1) * width, :],
+                in0=v_raw[head][:, PACK * g : PACK * (g + 1), part * width : (part + 1) * width].rearrange(
+                    "p t d -> p d t"
+                ),
+                scalar1=1.0,
+                scalar2=0.0,
+                op0=ALU.mult,
+                op1=ALU.add,
+            )
+
+        def quantise_v(head):
+            v_words[head] = operands.tile([P, PASSES, D], U32, name="v_words", align_bytes=64)
+            v_scales[head] = operands.tile([P, PASSES, D], U8, name="v_scales", align_bytes=64)
+            nc.vector.quantize_mx(
+                out=v_words[head][:].rearrange("p g d -> p (g d)").bitcast(FP8X4),
+                scales=v_scales[head][:].rearrange("p g d -> p (g d)"),
+                in_=v_grouped[head][:].rearrange("p g d t -> p (g d t)"),
+            )
+
+        def scores(j, key_half):
+            head, i = divmod(j, TILES)
+            score[(j, key_half)] = score_banks.tile([P, BANK], F32, name="score")
+            for c in range(4):
+                u, member = divmod(c, 2)
+                nc.tensor.matmul(
+                    score[(j, key_half)][:],
+                    lhsT=q_t[head][:, i, u, :].bitcast(BF16).rearrange("p (q e) -> p q e", e=2)[:, :, member],
+                    rhs=k_t[head][:, u, key_half * BANK : (key_half + 1) * BANK]
+                    .bitcast(BF16)
+                    .rearrange("p (n e) -> p n e", e=2)[:, :, member],
+                    start=(c == 0),
+                    stop=(c == 3),
+                )
+
+        def add_bias(j, key_half):
+            head, i = divmod(j, TILES)
+            h = HEADS[head][1]
+            if key_half == 0:
+                neg_s[j] = work.tile([P, N], F32, name="neg_s")
+            keys = slice(key_half * BANK, (key_half + 1) * BANK)
+            nc.vector.scalar_tensor_tensor(
+                out=neg_s[j][:, keys].rearrange("q (t p) -> q t p", t=PACK),
+                in0=score[(j, key_half)][:].rearrange("q (t p) -> q t p", t=PACK),
+                scalar=neg_factor[:, h : h + 1],
+                in1=bias_sb[h][:, i, keys].rearrange("q (p t) -> q t p", t=PACK),
+                op0=ALU.mult,
+                op1=ALU.subtract,
+            )
+
+        def row_maximum(j):
+            neg_max[j] = columns.tile([P, 1], F32, name="neg_max")
+            nc.vector.tensor_reduce(out=neg_max[j][:], in_=neg_s[j][:], axis=AXIS.X, op=ALU.min)
+
+        def exponential(j):
+            e_bf[j] = work.tile([P, N], BF16, name="e_bf")
+            row_sum[j] = columns.tile([P, 1], F32, name="row_sum")
+            nc.scalar.activation(
+                out=e_bf[j][:], in_=neg_s[j][:], func=ACT.Exp, bias=neg_max[j][:], scale=-1.0, accum_out=row_sum[j][:]
+            )
+
+        def transpose_e(j):
+            e_bank[j] = transpose_banks.tile([P, PASSES * PACK, P], BF16, name="e_bank", tag="bank")
+            for block in range(PASSES * PACK):
+                nc.tensor.transpose(e_bank[j][:, block, :], e_bf[j][:, block * P : (block + 1) * P], identity_bf16[:])
+
+        def regroup_e(j):
+            e_grouped[j] = work.tile([P, PASSES, P, PACK], BF16, name="e_grouped", align_bytes=64)
+            nc.scalar.copy(out=e_grouped[j][:], in_=e_bank[j][:].rearrange("p (g t) q -> p g q t", t=PACK))
+
+        def quantise_e(j):
+            e_words[j] = work.tile([P, PASSES * P], U32, name="e_words", align_bytes=64)
+            e_scales[j] = work.tile([P, PASSES * P], U8, name="e_scales", align_bytes=64)
+            nc.vector.quantize_mx(
+                out=e_words[j][:].bitcast(FP8X4),
+                scales=e_scales[j][:],
+                in_=e_grouped[j][:].rearrange("p g q t -> p (g q t)"),
+            )
+            inv_sum[j] = columns.tile([P, 1], F32, name="inv_sum")
+            nc.vector.reciprocal(out=inv_sum[j][:], in_=row_sum[j][:])
+
+        def mx_passes(j):
+            head = j // TILES
+            x_bank[j] = output_banks.tile([P, D], F32, name="x_bank")
+            for g in range(PASSES):
+                queries = slice(g * P, (g + 1) * P)
+                nc.tensor.matmul_mx(
+                    out=x_bank[j][:],
+                    lhsT=e_words[j][:, queries].bitcast(FP8X4),
+                    lhsT_scale=e_scales[j][:, queries],
+                    rhs=v_words[head][:, g, :].bitcast(FP8X4),
+                    rhs_scale=v_scales[head][:, g, :],
+                    start=(g == 0),
+                    stop=(g == PASSES - 1),
+                )
+
+        def output(j):
+            head, i = divmod(j, TILES)
+            b, h = HEADS[head]
+            x_sb = work.tile([P, D], F32, name="x_sb")
+            nc.scalar.activation(out=x_sb[:], in_=x_bank[j][:], func=ACT.Copy, scale=inv_sum[j][:])
+            row0 = b * N + i * P
+            nc.sync.dma_start(
+                out=out_rows[row0 : row0 + P, h : h + 1, :], in_=x_sb[:].rearrange("p (o d) -> p o d", o=1)
+            )
+
+        identity_bf16 = const.tile([P, P], BF16, name="identity_bf16")
+        make_identity(nc, identity_bf16[:])
+        identity_f32 = const.tile([P, P], F32, name="identity_f32")
+        make_identity(nc, identity_f32[:])
+        log_factor = const.tile([P, NHEADS], BF16, name="log_factor")
+        nc.sync.dma_start(out=log_factor[:], in_=logit_scale.rearrange("h a b -> (h a b)").partition_broadcast(P))
+        bias_sb = [const.tile([P, TILES, N], BF16, name="bias%d" % h) for h in range(NHEADS)]
+        new_head(0)
+        load_keys(k_raw[0], k_rows, first_row(0), 0, 4)
+        load_blocks(q_raw[0], q_rows, first_row(0), 0, 2)
+        load_keys(k_raw[0], k_rows, first_row(0), 4, 4)
+        load_blocks(bias_sb[0], bias_rows, 0, 0, 1)
+        load_keys(v_raw[0], v_rows, first_row(0), 0, TILES)
+        load_blocks(q_raw[0], q_rows, first_row(0), 2, 2)
+        load_blocks(bias_sb[0], bias_rows, 0, 1, 1)
+        load_blocks(q_raw[0], q_rows, first_row(0), 4, 4)
+        load_blocks(bias_sb[0], bias_rows, 0, 2, 2)
+        load_blocks(bias_sb[0], bias_rows, 0, 4, 4)
+
+        factor = const.tile([P, NHEADS], F32, name="factor")
+        nc.scalar.activation(out=factor[:], in_=log_factor[:], func=ACT.Exp)
+        neg_factor = const.tile([P, NHEADS], F32, name="neg_factor")
+        nc.vector.tensor_scalar(
+            out=neg_factor[:], in0=factor[:], scalar1=100.0, scalar2=-1.0, op0=ALU.min, op1=ALU.mult
+        )
+
+        for position, unit in enumerate(UNITS_BEFORE_A_HEAD):
+            unit_transposes(0, unit)
+            unit_copy(0, unit, on_vector=(position % 2 == 0))
+        for piece in range(V_PIECES):
+            regroup_v(0, piece)
+
+        def is_tile(j):
+            return 0 <= j < ALL_TILES
+
+        for step in range(ALL_TILES + MX_LAG):
+            head, i = divmod(step, TILES)
+            prepare = head + 1
+            preparing = is_tile(step) and prepare < len(HEADS)
+
+            if preparing and i == 0:
+                new_head(prepare)
+                load_keys(k_raw[prepare], k_rows, first_row(prepare), 0, TILES)
+            if preparing and i == 1:
+                load_blocks(q_raw[prepare], q_rows, first_row(prepare), 0, TILES)
+            if preparing and i == 2:
+                load_keys(v_raw[prepare], v_rows, first_row(prepare), 0, TILES)
+            if step == 3:
+                load_blocks(bias_sb[1], bias_rows, N, 0, TILES)
+
+            if i < len(UNITS_IN_A_HEAD):
+                unit_head, unit = head, UNITS_IN_A_HEAD[i]
+            else:
+                unit_head, unit = prepare, UNITS_BEFORE_A_HEAD[i - len(UNITS_IN_A_HEAD)]
+            has_unit = is_tile(step) and unit_head < len(HEADS)
+
+            if is_tile(step):
+                scores(step, 0)
+            if is_tile(step - MX_LAG):
+                mx_passes(step - MX_LAG)
+            if is_tile(step):
+                scores(step, 1)
+            if is_tile(step - TRANSPOSE_LAG):
+                transpose_e(step - TRANSPOSE_LAG)
+            if has_unit:
+                unit_transposes(unit_head, unit)
+
+            if is_tile(step):
+                add_bias(step, 0)
+            if is_tile(step - QUANTISE_LAG):
+                quantise_e(step - QUANTISE_LAG)
+            if is_tile(step):
+                add_bias(step, 1)
+                row_maximum(step)
+            if step == MX_LAG - 2:
+                quantise_v(0)
+            if preparing and i == TILES - 1:
+                quantise_v(prepare)
+
+            if is_tile(step - EXP_LAG):
+                exponential(step - EXP_LAG)
+            if is_tile(step - MX_LAG):
+                output(step - MX_LAG)
+            if is_tile(step - TRANSPOSE_LAG):
+                regroup_e(step - TRANSPOSE_LAG)
+            if has_unit:
+                unit_copy(unit_head, unit, on_vector=False)
+
+            first_piece = (i - V_FIRST_STEP) * V_PIECES_A_STEP
+            if preparing and 0 <= first_piece < V_PIECES:
+                for piece in range(first_piece, first_piece + V_PIECES_A_STEP):
+                    regroup_v(prepare, piece)

@@ -171,17 +171,27 @@ def tile_attention_pa_t_kernel(tc, q_hat, k_hat, v, logit_scale, bias, out):
             e_bf[j] = work.tile([P, N], BF16, name="e_bf")
             row_sum[j] = columns.tile([P, 1], F32, name="row_sum")
             nc.scalar.activation(
-                out=e_bf[j][:], in_=neg_s[j][:], func=ACT.Exp, bias=neg_max[j][:], scale=-1.0, accum_out=row_sum[j][:]
+                out=e_bf[j][:].rearrange("q (b p e) -> q b p e", p=P, e=2),
+                in_=neg_s[j][:].rearrange("q (b e p) -> q b p e", p=P, e=2),
+                func=ACT.Exp,
+                bias=neg_max[j][:],
+                scale=-1.0,
+                accum_out=row_sum[j][:],
             )
 
         def transpose_e(j):
-            e_bank[j] = transpose_banks.tile([P, PASSES * PACK, P], BF16, name="e_bank", tag="bank")
-            for block in range(PASSES * PACK):
-                nc.tensor.transpose(e_bank[j][:, block, :], e_bf[j][:, block * P : (block + 1) * P], identity_bf16[:])
+            e_bank[j] = transpose_banks.tile([P, 2 * PASSES, P], F32, name="e_bank", tag="bank")
+            for block in range(2 * PASSES):
+                nc.tensor.transpose(
+                    e_bank[j][:, block, :], e_bf[j][:, 2 * block * P : 2 * (block + 1) * P].bitcast(F32), identity_f32[:]
+                )
 
         def regroup_e(j):
             e_grouped[j] = work.tile([P, PASSES, P, PACK], BF16, name="e_grouped", align_bytes=64)
-            nc.scalar.copy(out=e_grouped[j][:], in_=e_bank[j][:].rearrange("p (g t) q -> p g q t", t=PACK))
+            nc.scalar.copy(
+                out=e_grouped[j][:].rearrange("p g q t -> p (g q t)").bitcast(F32).rearrange("p (g q u) -> p g q u", q=P, u=2),
+                in_=e_bank[j][:].rearrange("p (g u) q -> p g q u", u=2),
+            )
 
         def quantise_e(j):
             e_words[j] = work.tile([P, PASSES * P], U32, name="e_words", align_bytes=64)
@@ -219,8 +229,6 @@ def tile_attention_pa_t_kernel(tc, q_hat, k_hat, v, logit_scale, bias, out):
                 out=out_rows[row0 : row0 + P, h : h + 1, :], in_=x_sb[:].rearrange("p (o d) -> p o d", o=1)
             )
 
-        identity_bf16 = const.tile([P, P], BF16, name="identity_bf16")
-        make_identity(nc, identity_bf16[:])
         identity_f32 = const.tile([P, P], F32, name="identity_f32")
         make_identity(nc, identity_f32[:])
         log_factor = const.tile([P, NHEADS], BF16, name="log_factor")

@@ -26,6 +26,8 @@ EXP_LAG = 1
 TRANSPOSE_LAG = 2
 QUANTISE_LAG = 3
 MX_LAG = 4
+LAST = ALL_TILES - 1
+FIRST_LATE_TILE = ALL_TILES - MX_LAG
 
 UNITS_BEFORE_A_HEAD = (0, 1, 4, 2, 3)
 UNITS_IN_A_HEAD = (5, 6, 7)
@@ -135,7 +137,7 @@ def tile_attention_pa_t_kernel(tc, q_hat, k_hat, v, logit_scale, bias, out):
 
         def scores(j, key_half):
             head, i = divmod(j, TILES)
-            score[(j, key_half)] = score_banks.tile([P, BANK], F32, name="score")
+            score[(j, key_half)] = score_banks.tile([P, BANK], F32, name="score", tag="score")
             for c in range(4):
                 u, member = divmod(c, 2)
                 nc.tensor.matmul(
@@ -201,12 +203,17 @@ def tile_attention_pa_t_kernel(tc, q_hat, k_hat, v, logit_scale, bias, out):
                 scales=e_scales[j][:],
                 in_=e_grouped[j][:].rearrange("p g q t -> p (g q t)"),
             )
+
+        def invert_sum(j):
             inv_sum[j] = columns.tile([P, 1], F32, name="inv_sum")
             nc.vector.reciprocal(out=inv_sum[j][:], in_=row_sum[j][:])
 
         def mx_passes(j):
             head = j // TILES
-            x_bank[j] = output_banks.tile([P, D], F32, name="x_bank")
+            if j < FIRST_LATE_TILE:
+                x_bank[j] = output_banks.tile([P, D], F32, name="x_bank")
+            else:
+                x_bank[j] = score_banks.tile([P, D], F32, name="late_x_bank", tag="score")
             for g in range(PASSES):
                 queries = slice(g * P, (g + 1) * P)
                 nc.tensor.matmul_mx(
@@ -219,15 +226,89 @@ def tile_attention_pa_t_kernel(tc, q_hat, k_hat, v, logit_scale, bias, out):
                     stop=(g == PASSES - 1),
                 )
 
-        def output(j):
+        def normalise(dst, src, inverse, on_vector):
+            if on_vector:
+                nc.vector.tensor_scalar(out=dst, in0=src, scalar1=inverse, scalar2=None, op0=ALU.mult)
+            else:
+                nc.scalar.activation(out=dst, in_=src, func=ACT.Copy, scale=inverse)
+
+        def store(j, x_sb, columns_of_d):
             head, i = divmod(j, TILES)
             b, h = HEADS[head]
-            x_sb = work.tile([P, D], F32, name="x_sb")
-            nc.scalar.activation(out=x_sb[:], in_=x_bank[j][:], func=ACT.Copy, scale=inv_sum[j][:])
             row0 = b * N + i * P
             nc.sync.dma_start(
-                out=out_rows[row0 : row0 + P, h : h + 1, :], in_=x_sb[:].rearrange("p (o d) -> p o d", o=1)
+                out=out_rows[row0 : row0 + P, h : h + 1, columns_of_d], in_=x_sb[:].rearrange("p (o d) -> p o d", o=1)
             )
+
+        def output(j, on_vector=False):
+            x_sb = work.tile([P, D], F32, name="x_sb")
+            normalise(x_sb[:], x_bank[j][:], inv_sum[j][:], on_vector)
+            store(j, x_sb, slice(0, D))
+
+        half_max, half_sum, half_e, half_bank, half_grouped, half_words, half_scales = {}, {}, {}, {}, {}, {}, {}
+
+        def half_maximum(j, g):
+            if g == 0:
+                half_max[j] = columns.tile([P, PASSES], F32, name="half_max")
+            nc.vector.tensor_reduce(
+                out=half_max[j][:, g : g + 1], in_=neg_s[j][:, g * BANK : (g + 1) * BANK], axis=AXIS.X, op=ALU.min
+            )
+
+        def join_maximum(j):
+            neg_max[j] = columns.tile([P, 1], F32, name="neg_max")
+            nc.vector.tensor_reduce(out=neg_max[j][:], in_=half_max[j][:], axis=AXIS.X, op=ALU.min)
+
+        def half_exponential(j, g):
+            if g == 0:
+                half_sum[j] = columns.tile([P, PASSES], F32, name="half_sum")
+            half_e[g] = work.tile([P, BANK], BF16, name="half_e")
+            nc.scalar.activation(
+                out=half_e[g][:].rearrange("q (b p e) -> q b p e", p=P, e=2),
+                in_=neg_s[j][:, g * BANK : (g + 1) * BANK].rearrange("q (b e p) -> q b p e", p=P, e=2),
+                func=ACT.Exp,
+                bias=neg_max[j][:],
+                scale=-1.0,
+                accum_out=half_sum[j][:, g : g + 1],
+            )
+
+        def half_transpose(g):
+            half_bank[g] = transpose_banks.tile([P, 2, P], F32, name="half_bank", tag="bank")
+            for u in range(2):
+                nc.tensor.transpose(
+                    half_bank[g][:, u, :], half_e[g][:, 2 * u * P : 2 * (u + 1) * P].bitcast(F32), identity_f32[:]
+                )
+
+        def half_regroup(g, on_vector):
+            half_grouped[g] = work.tile([P, P * PACK], BF16, name="half_grouped", align_bytes=64)
+            dst = half_grouped[g][:].bitcast(F32).rearrange("p (q u) -> p q u", u=2)
+            src = half_bank[g][:].rearrange("p u q -> p q u")
+            if on_vector:
+                nc.vector.tensor_copy(out=dst, in_=src)
+            else:
+                nc.scalar.copy(out=dst, in_=src)
+
+        def half_quantise(g):
+            half_words[g] = work.tile([P, P], U32, name="half_words", align_bytes=64)
+            half_scales[g] = work.tile([P, P], U8, name="half_scales", align_bytes=64)
+            nc.vector.quantize_mx(out=half_words[g][:].bitcast(FP8X4), scales=half_scales[g][:], in_=half_grouped[g][:])
+
+        def join_sum(j):
+            row_sum[j] = columns.tile([P, 1], F32, name="row_sum")
+            nc.vector.tensor_reduce(out=row_sum[j][:], in_=half_sum[j][:], axis=AXIS.X, op=ALU.add)
+
+        def half_mx_pass(j, banks, g):
+            head = j // TILES
+            for half, bank in enumerate(banks):
+                part = slice(half * D // 2, (half + 1) * D // 2)
+                nc.tensor.matmul_mx(
+                    out=bank[:, : D // 2],
+                    lhsT=half_words[g][:].bitcast(FP8X4),
+                    lhsT_scale=half_scales[g][:],
+                    rhs=v_words[head][:, g, part].bitcast(FP8X4),
+                    rhs_scale=v_scales[head][:, g, part],
+                    start=(g == 0),
+                    stop=(g == PASSES - 1),
+                )
 
         identity_f32 = const.tile([P, P], F32, name="identity_f32")
         make_identity(nc, identity_f32[:])
@@ -262,10 +343,10 @@ def tile_attention_pa_t_kernel(tc, q_hat, k_hat, v, logit_scale, bias, out):
         def is_tile(j):
             return 0 <= j < ALL_TILES
 
-        for step in range(ALL_TILES + MX_LAG):
+        for step in range(ALL_TILES):
             head, i = divmod(step, TILES)
             prepare = head + 1
-            preparing = is_tile(step) and prepare < len(HEADS)
+            preparing = prepare < len(HEADS)
 
             if preparing and i == 0:
                 new_head(prepare)
@@ -281,25 +362,29 @@ def tile_attention_pa_t_kernel(tc, q_hat, k_hat, v, logit_scale, bias, out):
                 unit_head, unit = head, UNITS_IN_A_HEAD[i]
             else:
                 unit_head, unit = prepare, UNITS_BEFORE_A_HEAD[i - len(UNITS_IN_A_HEAD)]
-            has_unit = is_tile(step) and unit_head < len(HEADS)
+            has_unit = unit_head < len(HEADS)
 
-            if is_tile(step):
-                scores(step, 0)
+            scores(step, 0)
             if is_tile(step - MX_LAG):
                 mx_passes(step - MX_LAG)
-            if is_tile(step):
-                scores(step, 1)
+            scores(step, 1)
             if is_tile(step - TRANSPOSE_LAG):
                 transpose_e(step - TRANSPOSE_LAG)
             if has_unit:
                 unit_transposes(unit_head, unit)
 
-            if is_tile(step):
-                add_bias(step, 0)
+            add_bias(step, 0)
             if is_tile(step - QUANTISE_LAG):
                 quantise_e(step - QUANTISE_LAG)
-            if is_tile(step):
-                add_bias(step, 1)
+            if step == LAST:
+                half_maximum(step, 0)
+            add_bias(step, 1)
+            if is_tile(step - QUANTISE_LAG):
+                invert_sum(step - QUANTISE_LAG)
+            if step == LAST:
+                half_maximum(step, 1)
+                join_maximum(step)
+            else:
                 row_maximum(step)
             if step == MX_LAG - 2:
                 quantise_v(0)
@@ -308,7 +393,7 @@ def tile_attention_pa_t_kernel(tc, q_hat, k_hat, v, logit_scale, bias, out):
 
             if is_tile(step - EXP_LAG):
                 exponential(step - EXP_LAG)
-            if is_tile(step - MX_LAG):
+            if is_tile(step - MX_LAG) and step < LAST:
                 output(step - MX_LAG)
             if is_tile(step - TRANSPOSE_LAG):
                 regroup_e(step - TRANSPOSE_LAG)
@@ -319,3 +404,34 @@ def tile_attention_pa_t_kernel(tc, q_hat, k_hat, v, logit_scale, bias, out):
             if preparing and 0 <= first_piece < V_PIECES:
                 for piece in range(first_piece, first_piece + V_PIECES_A_STEP):
                     regroup_v(prepare, piece)
+
+        mx_passes(LAST - 3)
+        transpose_e(LAST - 1)
+        regroup_e(LAST - 1)
+        half_exponential(LAST, 0)
+        half_exponential(LAST, 1)
+        quantise_e(LAST - 2)
+        mx_passes(LAST - 2)
+        quantise_e(LAST - 1)
+        invert_sum(LAST - 2)
+        invert_sum(LAST - 1)
+        output(LAST - 4, on_vector=True)
+        output(LAST - 3, on_vector=False)
+        half_transpose(0)
+        half_transpose(1)
+        mx_passes(LAST - 1)
+        late_banks = [score_banks.tile([P, D], F32, name="half_x_bank", tag="score") for half in range(2)]
+        half_regroup(0, on_vector=True)
+        half_quantise(0)
+        half_mx_pass(LAST, late_banks, 0)
+        half_regroup(1, on_vector=False)
+        join_sum(LAST)
+        half_quantise(1)
+        half_mx_pass(LAST, late_banks, 1)
+        invert_sum(LAST)
+        output(LAST - 2, on_vector=True)
+        output(LAST - 1, on_vector=False)
+        for half in range(2):
+            x_sb = work.tile([P, D // 2], F32, name="half_x_sb")
+            normalise(x_sb[:], late_banks[half][:, : D // 2], inv_sum[LAST][:], on_vector=(half == 0))
+            store(LAST, x_sb, slice(half * D // 2, (half + 1) * D // 2))

@@ -36,6 +36,8 @@ V_PIECES = 8
 V_PIECES_A_STEP = 2
 V_FIRST_STEP = 3
 
+WARM_UP = 6
+
 
 def tile_attention_pa_t_kernel(tc, q_hat, k_hat, v, logit_scale, bias, out):
     nc = tc.nc
@@ -86,10 +88,11 @@ def tile_attention_pa_t_kernel(tc, q_hat, k_hat, v, logit_scale, bias, out):
             q_t[head] = operands.tile([P, TILES, 2, P], F32, name="q_t")
             k_t[head] = operands.tile([P, 2, N], F32, name="k_t")
 
-        def unit_transposes(head, unit):
-            bank = transpose_banks.tile([P, 4, P], F32, name="unit_bank", tag="bank")
-            unit_bank[(head, unit)] = bank
-            for m in range(4):
+        def unit_transposes(head, unit, members=range(4)):
+            if members[0] == 0:
+                unit_bank[(head, unit)] = transpose_banks.tile([P, 4, P], F32, name="unit_bank", tag="bank")
+            bank = unit_bank[(head, unit)]
+            for m in members:
                 if unit < 4:
                     key_half, u = divmod(unit, 2)
                     src = k_raw[head][:, 4 * key_half + m, 2 * u * P : 2 * (u + 1) * P]
@@ -98,13 +101,14 @@ def tile_attention_pa_t_kernel(tc, q_hat, k_hat, v, logit_scale, bias, out):
                     src = q_raw[head][:, 2 * (unit - 4) + tile_in_pair, 2 * u * P : 2 * (u + 1) * P]
                 nc.tensor.transpose(bank[:, m, :], src.bitcast(F32), identity_f32[:])
 
-        def unit_copy(head, unit, on_vector):
+        def unit_copy(head, unit, on_vector, members=range(4)):
             if unit < 4:
                 key_half, u = divmod(unit, 2)
                 dst = k_t[head][:, u, key_half * BANK : (key_half + 1) * BANK]
             else:
-                dst = q_t[head][:, 2 * (unit - 4) : 2 * (unit - 3), :, :].rearrange("p i u q -> p (i u q)")
-            src = unit_bank[(head, unit)][:].rearrange("p m c -> p (m c)")
+                tiles = slice(2 * (unit - 4) + members[0] // 2, 2 * (unit - 4) + (members[-1] + 1) // 2)
+                dst = q_t[head][:, tiles, :, :].rearrange("p i u q -> p (i u q)")
+            src = unit_bank[(head, unit)][:, members[0] : members[-1] + 1, :].rearrange("p m c -> p (m c)")
             if on_vector:
                 nc.vector.tensor_copy(out=dst, in_=src)
             else:
@@ -135,10 +139,11 @@ def tile_attention_pa_t_kernel(tc, q_hat, k_hat, v, logit_scale, bias, out):
                 in_=v_grouped[head][:].rearrange("p g d t -> p (g d t)"),
             )
 
-        def scores(j, key_half):
+        def scores(j, key_half, chunks=range(4)):
             head, i = divmod(j, TILES)
-            score[(j, key_half)] = score_banks.tile([P, BANK], F32, name="score", tag="score")
-            for c in range(4):
+            if chunks[0] == 0:
+                score[(j, key_half)] = score_banks.tile([P, BANK], F32, name="score", tag="score")
+            for c in chunks:
                 u, member = divmod(c, 2)
                 nc.tensor.matmul(
                     score[(j, key_half)][:],
@@ -154,7 +159,7 @@ def tile_attention_pa_t_kernel(tc, q_hat, k_hat, v, logit_scale, bias, out):
             head, i = divmod(j, TILES)
             h = HEADS[head][1]
             if key_half == 0:
-                neg_s[j] = work.tile([P, N], F32, name="neg_s")
+                neg_s[j] = work.tile([P, N + 1], F32, name="neg_s")
             keys = slice(key_half * BANK, (key_half + 1) * BANK)
             nc.vector.scalar_tensor_tensor(
                 out=neg_s[j][:, keys].rearrange("q (t p) -> q t p", t=PACK),
@@ -167,14 +172,14 @@ def tile_attention_pa_t_kernel(tc, q_hat, k_hat, v, logit_scale, bias, out):
 
         def row_maximum(j):
             neg_max[j] = columns.tile([P, 1], F32, name="neg_max")
-            nc.vector.tensor_reduce(out=neg_max[j][:], in_=neg_s[j][:], axis=AXIS.X, op=ALU.min)
+            nc.vector.tensor_reduce(out=neg_max[j][:], in_=neg_s[j][:, :N], axis=AXIS.X, op=ALU.min)
 
         def exponential(j):
             e_bf[j] = work.tile([P, N], BF16, name="e_bf")
             row_sum[j] = columns.tile([P, 1], F32, name="row_sum")
             nc.scalar.activation(
                 out=e_bf[j][:].rearrange("q (b p e) -> q b p e", p=P, e=2),
-                in_=neg_s[j][:].rearrange("q (b e p) -> q b p e", p=P, e=2),
+                in_=neg_s[j][:, :N].rearrange("q (b e p) -> q b p e", p=P, e=2),
                 func=ACT.Exp,
                 bias=neg_max[j][:],
                 scale=-1.0,
@@ -232,11 +237,11 @@ def tile_attention_pa_t_kernel(tc, q_hat, k_hat, v, logit_scale, bias, out):
             else:
                 nc.scalar.activation(out=dst, in_=src, func=ACT.Copy, scale=inverse)
 
-        def store(j, x_sb, columns_of_d):
+        def store(j, x_sb, columns_of_d, queue=nc.sync):
             head, i = divmod(j, TILES)
             b, h = HEADS[head]
             row0 = b * N + i * P
-            nc.sync.dma_start(
+            queue.dma_start(
                 out=out_rows[row0 : row0 + P, h : h + 1, columns_of_d], in_=x_sb[:].rearrange("p (o d) -> p o d", o=1)
             )
 
@@ -245,18 +250,14 @@ def tile_attention_pa_t_kernel(tc, q_hat, k_hat, v, logit_scale, bias, out):
             normalise(x_sb[:], x_bank[j][:], inv_sum[j][:], on_vector)
             store(j, x_sb, slice(0, D))
 
-        half_max, half_sum, half_e, half_bank, half_grouped, half_words, half_scales = {}, {}, {}, {}, {}, {}, {}
+        half_sum, half_e, half_bank, half_grouped, half_words, half_scales, half_x_bank = {}, {}, {}, {}, {}, {}, {}
 
-        def half_maximum(j, g):
-            if g == 0:
-                half_max[j] = columns.tile([P, PASSES], F32, name="half_max")
-            nc.vector.tensor_reduce(
-                out=half_max[j][:, g : g + 1], in_=neg_s[j][:, g * BANK : (g + 1) * BANK], axis=AXIS.X, op=ALU.min
-            )
+        def first_half_maximum(j):
+            nc.vector.tensor_reduce(out=neg_s[j][:, N : N + 1], in_=neg_s[j][:, :BANK], axis=AXIS.X, op=ALU.min)
 
-        def join_maximum(j):
+        def second_half_maximum(j):
             neg_max[j] = columns.tile([P, 1], F32, name="neg_max")
-            nc.vector.tensor_reduce(out=neg_max[j][:], in_=half_max[j][:], axis=AXIS.X, op=ALU.min)
+            nc.vector.tensor_reduce(out=neg_max[j][:], in_=neg_s[j][:, BANK:], axis=AXIS.X, op=ALU.min)
 
         def half_exponential(j, g):
             if g == 0:
@@ -296,36 +297,72 @@ def tile_attention_pa_t_kernel(tc, q_hat, k_hat, v, logit_scale, bias, out):
             row_sum[j] = columns.tile([P, 1], F32, name="row_sum")
             nc.vector.tensor_reduce(out=row_sum[j][:], in_=half_sum[j][:], axis=AXIS.X, op=ALU.add)
 
-        def half_mx_pass(j, banks, g):
+        def mx_pass_by_halves(j, g, words, scales):
             head = j // TILES
-            for half, bank in enumerate(banks):
+            for half in range(2):
+                if g == 0:
+                    half_x_bank[(j, half)] = score_banks.tile([P, D], F32, name="half_x_bank", tag="score")
                 part = slice(half * D // 2, (half + 1) * D // 2)
                 nc.tensor.matmul_mx(
-                    out=bank[:, : D // 2],
-                    lhsT=half_words[g][:].bitcast(FP8X4),
-                    lhsT_scale=half_scales[g][:],
+                    out=half_x_bank[(j, half)][:, : D // 2],
+                    lhsT=words.bitcast(FP8X4),
+                    lhsT_scale=scales,
                     rhs=v_words[head][:, g, part].bitcast(FP8X4),
                     rhs_scale=v_scales[head][:, g, part],
                     start=(g == 0),
                     stop=(g == PASSES - 1),
                 )
 
+        def output_by_halves(j):
+            for half, queue in enumerate((nc.sync, nc.scalar)):
+                x_sb = work.tile([P, D // 2], F32, name="half_x_sb")
+                normalise(x_sb[:], half_x_bank[(j, half)][:, : D // 2], inv_sum[j][:], on_vector=(half == 0))
+                store(j, x_sb, slice(half * D // 2, (half + 1) * D // 2), queue)
+
+        zeros = const.tile([P, BANK], BF16, name="zeros")
+        nc.vector.memset(zeros[:], 0.0)
+
+        def warm_up(count):
+            bank = score_banks.tile([P, BANK], F32, name="warm_bank", tag="score")
+            for repeat in range(count):
+                nc.tensor.matmul(bank[:], lhsT=zeros[:, :P], rhs=zeros[:], start=True, stop=True)
+
         identity_f32 = const.tile([P, P], F32, name="identity_f32")
         make_identity(nc, identity_f32[:])
-        log_factor = const.tile([P, NHEADS], BF16, name="log_factor")
-        nc.sync.dma_start(out=log_factor[:], in_=logit_scale.rearrange("h a b -> (h a b)").partition_broadcast(P))
         bias_sb = [const.tile([P, TILES, N], BF16, name="bias%d" % h) for h in range(NHEADS)]
         new_head(0)
         load_keys(k_raw[0], k_rows, first_row(0), 0, 4)
-        load_blocks(q_raw[0], q_rows, first_row(0), 0, 2)
+        load_blocks(q_raw[0], q_rows, first_row(0), 0, 1)
         load_keys(k_raw[0], k_rows, first_row(0), 4, 4)
+        log_factor = const.tile([P, NHEADS], BF16, name="log_factor")
+        nc.sync.dma_start(out=log_factor[:], in_=logit_scale.rearrange("h a b -> (h a b)").partition_broadcast(P))
         load_blocks(bias_sb[0], bias_rows, 0, 0, 1)
+        load_blocks(q_raw[0], q_rows, first_row(0), 1, 3)
         load_keys(v_raw[0], v_rows, first_row(0), 0, TILES)
-        load_blocks(q_raw[0], q_rows, first_row(0), 2, 2)
         load_blocks(bias_sb[0], bias_rows, 0, 1, 1)
         load_blocks(q_raw[0], q_rows, first_row(0), 4, 4)
         load_blocks(bias_sb[0], bias_rows, 0, 2, 2)
         load_blocks(bias_sb[0], bias_rows, 0, 4, 4)
+
+        unread = const.tile([P, 1], F32, name="unread")
+        nc.scalar.activation(out=unread[:], in_=zeros[:, :1], func=ACT.Exp)
+
+        warm_up(WARM_UP)
+        unit_transposes(0, 0)
+        unit_copy(0, 0, on_vector=True)
+        unit_transposes(0, 1)
+        unit_copy(0, 1, on_vector=False)
+        unit_transposes(0, 4, members=range(2))
+        unit_copy(0, 4, on_vector=True, members=range(2))
+        warm_up(2)
+        scores(0, 0, chunks=range(2))
+        unit_transposes(0, 2)
+        unit_copy(0, 2, on_vector=False)
+        unit_transposes(0, 3)
+        unit_copy(0, 3, on_vector=True)
+        scores(0, 0, chunks=range(2, 4))
+        unit_transposes(0, 4, members=range(2, 4))
+        unit_copy(0, 4, on_vector=False, members=range(2, 4))
 
         factor = const.tile([P, NHEADS], F32, name="factor")
         nc.scalar.activation(out=factor[:], in_=log_factor[:], func=ACT.Exp)
@@ -333,10 +370,6 @@ def tile_attention_pa_t_kernel(tc, q_hat, k_hat, v, logit_scale, bias, out):
         nc.vector.tensor_scalar(
             out=neg_factor[:], in0=factor[:], scalar1=100.0, scalar2=-1.0, op0=ALU.min, op1=ALU.mult
         )
-
-        for position, unit in enumerate(UNITS_BEFORE_A_HEAD):
-            unit_transposes(0, unit)
-            unit_copy(0, unit, on_vector=(position % 2 == 0))
         for piece in range(V_PIECES):
             regroup_v(0, piece)
 
@@ -364,7 +397,8 @@ def tile_attention_pa_t_kernel(tc, q_hat, k_hat, v, logit_scale, bias, out):
                 unit_head, unit = prepare, UNITS_BEFORE_A_HEAD[i - len(UNITS_IN_A_HEAD)]
             has_unit = unit_head < len(HEADS)
 
-            scores(step, 0)
+            if step > 0:
+                scores(step, 0)
             if is_tile(step - MX_LAG):
                 mx_passes(step - MX_LAG)
             scores(step, 1)
@@ -377,13 +411,12 @@ def tile_attention_pa_t_kernel(tc, q_hat, k_hat, v, logit_scale, bias, out):
             if is_tile(step - QUANTISE_LAG):
                 quantise_e(step - QUANTISE_LAG)
             if step == LAST:
-                half_maximum(step, 0)
+                first_half_maximum(step)
             add_bias(step, 1)
             if is_tile(step - QUANTISE_LAG):
                 invert_sum(step - QUANTISE_LAG)
             if step == LAST:
-                half_maximum(step, 1)
-                join_maximum(step)
+                second_half_maximum(step)
             else:
                 row_maximum(step)
             if step == MX_LAG - 2:
@@ -393,7 +426,7 @@ def tile_attention_pa_t_kernel(tc, q_hat, k_hat, v, logit_scale, bias, out):
 
             if is_tile(step - EXP_LAG):
                 exponential(step - EXP_LAG)
-            if is_tile(step - MX_LAG) and step < LAST:
+            if is_tile(step - MX_LAG):
                 output(step - MX_LAG)
             if is_tile(step - TRANSPOSE_LAG):
                 regroup_e(step - TRANSPOSE_LAG)
@@ -415,23 +448,20 @@ def tile_attention_pa_t_kernel(tc, q_hat, k_hat, v, logit_scale, bias, out):
         quantise_e(LAST - 1)
         invert_sum(LAST - 2)
         invert_sum(LAST - 1)
-        output(LAST - 4, on_vector=True)
-        output(LAST - 3, on_vector=False)
+        output(LAST - 3, on_vector=True)
+        output(LAST - 2, on_vector=False)
         half_transpose(0)
         half_transpose(1)
-        mx_passes(LAST - 1)
-        late_banks = [score_banks.tile([P, D], F32, name="half_x_bank", tag="score") for half in range(2)]
+        for g in range(PASSES):
+            queries = slice(g * P, (g + 1) * P)
+            mx_pass_by_halves(LAST - 1, g, e_words[LAST - 1][:, queries], e_scales[LAST - 1][:, queries])
+        join_sum(LAST)
         half_regroup(0, on_vector=True)
         half_quantise(0)
-        half_mx_pass(LAST, late_banks, 0)
         half_regroup(1, on_vector=False)
-        join_sum(LAST)
         half_quantise(1)
-        half_mx_pass(LAST, late_banks, 1)
+        for g in range(PASSES):
+            mx_pass_by_halves(LAST, g, half_words[g][:], half_scales[g][:])
         invert_sum(LAST)
-        output(LAST - 2, on_vector=True)
-        output(LAST - 1, on_vector=False)
-        for half in range(2):
-            x_sb = work.tile([P, D // 2], F32, name="half_x_sb")
-            normalise(x_sb[:], late_banks[half][:, : D // 2], inv_sum[LAST][:], on_vector=(half == 0))
-            store(LAST, x_sb, slice(half * D // 2, (half + 1) * D // 2))
+        output_by_halves(LAST - 1)
+        output_by_halves(LAST)

@@ -30,11 +30,17 @@ LAST = ALL_TILES - 1
 FIRST_LATE_TILE = ALL_TILES - MX_LAG
 
 UNITS_BEFORE_A_HEAD = (0, 1, 4, 2, 3)
-UNITS_IN_A_HEAD = (5, 6, 7)
+UNITS_IN_A_HEAD = ((5, 6, 7), (5,), (5,), (5,))
+FIRST_UNIT_STEP = (3, 3, 3, 3)
+FIRST_TURN_STEP = 4
+BLOCK = 32
+TURNED = 4
+TURNS = 2 * (TILES - TURNED)
 
 V_PIECES = 8
-V_PIECES_A_STEP = 2
-V_FIRST_STEP = 3
+V_PARTS = 4
+V_PIECES_A_PART = V_PIECES // V_PARTS
+V_FIRST_STEP = 5
 
 WARM_UP = 6
 
@@ -54,11 +60,13 @@ def tile_attention_pa_t_kernel(tc, q_hat, k_hat, v, logit_scale, bias, out):
         work = ctx.enter_context(tc.tile_pool(name="work", bufs=4))
         columns = ctx.enter_context(tc.tile_pool(name="columns", bufs=8))
         score_banks = ctx.enter_context(tc.psum_pool(name="score_banks", bufs=4))
-        transpose_banks = ctx.enter_context(tc.psum_pool(name="transpose_banks", bufs=3))
-        output_banks = ctx.enter_context(tc.psum_pool(name="output_banks", bufs=1))
+        transpose_banks = ctx.enter_context(tc.psum_pool(name="transpose_banks", bufs=2))
+        output_banks = ctx.enter_context(tc.psum_pool(name="output_banks", bufs=2))
         ctx.enter_context(tc.manual_schedule())
 
-        q_raw, k_raw, v_raw, q_t, k_t, v_grouped, v_words, v_scales, unit_bank = {}, {}, {}, {}, {}, {}, {}, {}, {}
+        q_raw, q_blocks, k_raw, v_raw, q_t, k_t, v_grouped, v_words, v_scales, unit_bank = (
+            {}, {}, {}, {}, {}, {}, {}, {}, {}, {},
+        )
         score, neg_s, neg_max, row_sum, inv_sum, e_bf, e_bank, e_grouped, e_words, e_scales, x_bank = (
             {}, {}, {}, {}, {}, {}, {}, {}, {}, {}, {},
         )
@@ -81,15 +89,28 @@ def tile_attention_pa_t_kernel(tc, q_hat, k_hat, v, logit_scale, bias, out):
                 in_=rows[row0 + first * P : row0 + (first + count) * P, :].rearrange("(t p) d -> p t d", p=P),
             )
 
+        def load_queries(head):
+            rows = slice(first_row(head) + TURNED * P, first_row(head) + N)
+            q_blocks[head] = raw.tile([P, 2, (N - TURNED * P) // BLOCK, 2 * BLOCK], BF16, name="q_blocks", align_bytes=64)
+            for u in range(2):
+                for quadrant in range(P // BLOCK):
+                    column = 2 * (u * P + quadrant * BLOCK)
+                    nc.sync.dma_start(
+                        out=q_blocks[head][quadrant * BLOCK : (quadrant + 1) * BLOCK, u, :, :],
+                        in_=q_rows[rows, column : column + 2 * BLOCK].rearrange("(b r) c -> r b c", r=BLOCK),
+                    )
+
         def new_head(head):
             q_raw[head] = raw.tile([P, TILES, D], BF16, name="q_raw")
             k_raw[head] = raw.tile([P, TILES, D], BF16, name="k_raw")
             v_raw[head] = raw.tile([P, TILES, D], BF16, name="v_raw")
-            q_t[head] = operands.tile([P, TILES, 2, P], F32, name="q_t")
+            q_t[head] = operands.tile([P, TILES, 2, P], F32, name="q_t", align_bytes=64)
             k_t[head] = operands.tile([P, 2, N], F32, name="k_t")
 
-        def unit_transposes(head, unit, members=range(4)):
-            if members[0] == 0:
+        def unit_transposes(head, unit, members=range(4), in_output_bank=False):
+            if members[0] == 0 and in_output_bank:
+                unit_bank[(head, unit)] = output_banks.tile([P, 4, P], F32, name="early_unit_bank", tag="x_bank")
+            elif members[0] == 0:
                 unit_bank[(head, unit)] = transpose_banks.tile([P, 4, P], F32, name="unit_bank", tag="bank")
             bank = unit_bank[(head, unit)]
             for m in members:
@@ -114,6 +135,16 @@ def tile_attention_pa_t_kernel(tc, q_hat, k_hat, v, logit_scale, bias, out):
             else:
                 nc.scalar.copy(out=dst, in_=src)
 
+        def turn_queries(head, turn):
+            tile_turned, u = divmod(turn, 2)
+            blocks = P // BLOCK
+            nc.vector.transpose(
+                q_t[head][:, TURNED + tile_turned, u, :],
+                q_blocks[head][:, u, tile_turned * blocks : (tile_turned + 1) * blocks, :]
+                .rearrange("p b c -> p (b c)")
+                .bitcast(F32),
+            )
+
         def regroup_v(head, piece):
             if piece == 0:
                 v_grouped[head] = operands.tile([P, PASSES, D, PACK], BF16, name="v_grouped", bufs=1, align_bytes=64)
@@ -130,13 +161,17 @@ def tile_attention_pa_t_kernel(tc, q_hat, k_hat, v, logit_scale, bias, out):
                 op1=ALU.add,
             )
 
-        def quantise_v(head):
-            v_words[head] = operands.tile([P, PASSES, D], U32, name="v_words", align_bytes=64)
-            v_scales[head] = operands.tile([P, PASSES, D], U8, name="v_scales", align_bytes=64)
+        def quantise_v(head, part):
+            if part == 0:
+                v_words[head] = operands.tile([P, PASSES, D], U32, name="v_words", align_bytes=64)
+                v_scales[head] = operands.tile([P, PASSES, D], U8, name="v_scales", align_bytes=64)
+            g, range_of_d = divmod(part, V_PARTS // PASSES)
+            width = D * PASSES // V_PARTS
+            columns_of_d = slice(range_of_d * width, (range_of_d + 1) * width)
             nc.vector.quantize_mx(
-                out=v_words[head][:].rearrange("p g d -> p (g d)").bitcast(FP8X4),
-                scales=v_scales[head][:].rearrange("p g d -> p (g d)"),
-                in_=v_grouped[head][:].rearrange("p g d t -> p (g d t)"),
+                out=v_words[head][:, g, columns_of_d].bitcast(FP8X4),
+                scales=v_scales[head][:, g, columns_of_d],
+                in_=v_grouped[head][:, g, columns_of_d, :].rearrange("p d t -> p (d t)"),
             )
 
         def scores(j, key_half, chunks=range(4)):
@@ -216,7 +251,7 @@ def tile_attention_pa_t_kernel(tc, q_hat, k_hat, v, logit_scale, bias, out):
         def mx_passes(j):
             head = j // TILES
             if j < FIRST_LATE_TILE:
-                x_bank[j] = output_banks.tile([P, D], F32, name="x_bank")
+                x_bank[j] = output_banks.tile([P, D], F32, name="x_bank", tag="x_bank")
             else:
                 x_bank[j] = score_banks.tile([P, D], F32, name="late_x_bank", tag="score")
             for g in range(PASSES):
@@ -352,11 +387,11 @@ def tile_attention_pa_t_kernel(tc, q_hat, k_hat, v, logit_scale, bias, out):
         unit_copy(0, 0, on_vector=True)
         unit_transposes(0, 1)
         unit_copy(0, 1, on_vector=False)
-        unit_transposes(0, 4, members=range(2))
+        unit_transposes(0, 4, members=range(2), in_output_bank=True)
         unit_copy(0, 4, on_vector=True, members=range(2))
         warm_up(2)
         scores(0, 0, chunks=range(2))
-        unit_transposes(0, 2)
+        unit_transposes(0, 2, in_output_bank=True)
         unit_copy(0, 2, on_vector=False)
         unit_transposes(0, 3)
         unit_copy(0, 3, on_vector=True)
@@ -385,17 +420,22 @@ def tile_attention_pa_t_kernel(tc, q_hat, k_hat, v, logit_scale, bias, out):
                 new_head(prepare)
                 load_keys(k_raw[prepare], k_rows, first_row(prepare), 0, TILES)
             if preparing and i == 1:
-                load_blocks(q_raw[prepare], q_rows, first_row(prepare), 0, TILES)
+                load_blocks(q_raw[prepare], q_rows, first_row(prepare), 0, TURNED)
+                load_queries(prepare)
             if preparing and i == 2:
                 load_keys(v_raw[prepare], v_rows, first_row(prepare), 0, TILES)
             if step == 3:
                 load_blocks(bias_sb[1], bias_rows, N, 0, TILES)
 
-            if i < len(UNITS_IN_A_HEAD):
-                unit_head, unit = head, UNITS_IN_A_HEAD[i]
-            else:
-                unit_head, unit = prepare, UNITS_BEFORE_A_HEAD[i - len(UNITS_IN_A_HEAD)]
-            has_unit = unit_head < len(HEADS)
+            unit = None
+            first = FIRST_UNIT_STEP[head]
+            if i < len(UNITS_IN_A_HEAD[head]):
+                unit_head, unit = head, UNITS_IN_A_HEAD[head][i]
+            elif preparing and first <= i < first + len(UNITS_BEFORE_A_HEAD):
+                unit_head, unit = prepare, UNITS_BEFORE_A_HEAD[i - first]
+            has_unit = unit is not None
+
+            turn_head, turn = divmod(step + TILES - FIRST_TURN_STEP, TILES)
 
             if step > 0:
                 scores(step, 0)
@@ -413,6 +453,8 @@ def tile_attention_pa_t_kernel(tc, q_hat, k_hat, v, logit_scale, bias, out):
             if step == LAST:
                 first_half_maximum(step)
             add_bias(step, 1)
+            if 0 < turn_head < len(HEADS):
+                turn_queries(turn_head, turn)
             if is_tile(step - QUANTISE_LAG):
                 invert_sum(step - QUANTISE_LAG)
             if step == LAST:
@@ -420,9 +462,11 @@ def tile_attention_pa_t_kernel(tc, q_hat, k_hat, v, logit_scale, bias, out):
             else:
                 row_maximum(step)
             if step == MX_LAG - 2:
-                quantise_v(0)
-            if preparing and i == TILES - 1:
-                quantise_v(prepare)
+                for part in range(V_PARTS):
+                    quantise_v(0, part)
+            v_head, part = divmod(step + TILES - V_FIRST_STEP - 1, TILES)
+            if 0 < v_head < len(HEADS) and part < V_PARTS:
+                quantise_v(v_head, part)
 
             if is_tile(step - EXP_LAG):
                 exponential(step - EXP_LAG)
@@ -433,10 +477,10 @@ def tile_attention_pa_t_kernel(tc, q_hat, k_hat, v, logit_scale, bias, out):
             if has_unit:
                 unit_copy(unit_head, unit, on_vector=False)
 
-            first_piece = (i - V_FIRST_STEP) * V_PIECES_A_STEP
-            if preparing and 0 <= first_piece < V_PIECES:
-                for piece in range(first_piece, first_piece + V_PIECES_A_STEP):
-                    regroup_v(prepare, piece)
+            v_head, part = divmod(step + TILES - V_FIRST_STEP, TILES)
+            if 0 < v_head < len(HEADS) and part < V_PARTS:
+                for piece in range(part * V_PIECES_A_PART, (part + 1) * V_PIECES_A_PART):
+                    regroup_v(v_head, piece)
 
         mx_passes(LAST - 3)
         transpose_e(LAST - 1)

@@ -30,19 +30,19 @@ LAST = ALL_TILES - 1
 FIRST_LATE_TILE = ALL_TILES - MX_LAG
 
 UNITS_BEFORE_A_HEAD = (0, 1, 4, 2, 3)
-UNITS_IN_A_HEAD = ((5, 6, 7), (5,), (5,), (5,))
-FIRST_UNIT_STEP = (3, 3, 3, 3)
-FIRST_TURN_STEP = 4
+FIRST_HEAD_UNITS = (5, 6, 7)
+FIRST_UNIT_STEP = TILES - len(UNITS_BEFORE_A_HEAD)
 BLOCK = 32
-TURNED = 4
-TURNS = 2 * (TILES - TURNED)
+TURNED = 2
+FIRST_TURN_STEP = 4
+TURNS_OF_STEP = (2, 2, 1, 1, 1, 1, 2, 2)
 
 V_PIECES = 8
 V_PARTS = 4
 V_PIECES_A_PART = V_PIECES // V_PARTS
 V_FIRST_STEP = 5
 
-WARM_UP = 6
+WARM_UP = 4
 
 
 def tile_attention_pa_t_kernel(tc, q_hat, k_hat, v, logit_scale, bias, out):
@@ -67,7 +67,7 @@ def tile_attention_pa_t_kernel(tc, q_hat, k_hat, v, logit_scale, bias, out):
         q_raw, q_blocks, k_raw, v_raw, q_t, k_t, v_grouped, v_words, v_scales, unit_bank = (
             {}, {}, {}, {}, {}, {}, {}, {}, {}, {},
         )
-        score, neg_s, neg_max, row_sum, inv_sum, e_bf, e_bank, e_grouped, e_words, e_scales, x_bank = (
+        score, neg_s, neg_max, row_sums, inv_sums, e_bf, e_bank, e_grouped, e_words, e_scales, x_bank = (
             {}, {}, {}, {}, {}, {}, {}, {}, {}, {}, {},
         )
 
@@ -81,6 +81,12 @@ def tile_attention_pa_t_kernel(tc, q_hat, k_hat, v, logit_scale, bias, out):
                 in_=rows[row0 + first * P : row0 + (first + count) * P, :].rearrange(
                     "(g p t) d -> p g t d", p=P, t=PACK
                 ),
+            )
+
+        def load_first_keys(dst, rows, row0, t0, count):
+            nc.sync.dma_start(
+                out=dst[:, t0 : t0 + count, :],
+                in_=rows[row0 : row0 + PACK * P, :].rearrange("(p t) d -> p t d", t=PACK)[:, t0 : t0 + count, :],
             )
 
         def load_blocks(dst, rows, row0, first, count):
@@ -161,17 +167,16 @@ def tile_attention_pa_t_kernel(tc, q_hat, k_hat, v, logit_scale, bias, out):
                 op1=ALU.add,
             )
 
-        def quantise_v(head, part):
-            if part == 0:
+        def quantise_v(head, first_part, count):
+            if first_part == 0:
                 v_words[head] = operands.tile([P, PASSES, D], U32, name="v_words", align_bytes=64)
                 v_scales[head] = operands.tile([P, PASSES, D], U8, name="v_scales", align_bytes=64)
-            g, range_of_d = divmod(part, V_PARTS // PASSES)
-            width = D * PASSES // V_PARTS
-            columns_of_d = slice(range_of_d * width, (range_of_d + 1) * width)
+            width = PASSES * D // V_PARTS
+            words = slice(first_part * width, (first_part + count) * width)
             nc.vector.quantize_mx(
-                out=v_words[head][:, g, columns_of_d].bitcast(FP8X4),
-                scales=v_scales[head][:, g, columns_of_d],
-                in_=v_grouped[head][:, g, columns_of_d, :].rearrange("p d t -> p (d t)"),
+                out=v_words[head][:].rearrange("p g d -> p (g d)")[:, words].bitcast(FP8X4),
+                scales=v_scales[head][:].rearrange("p g d -> p (g d)")[:, words],
+                in_=v_grouped[head][:].rearrange("p g d t -> p (g d t)")[:, PACK * words.start : PACK * words.stop],
             )
 
         def scores(j, key_half, chunks=range(4)):
@@ -209,16 +214,20 @@ def tile_attention_pa_t_kernel(tc, q_hat, k_hat, v, logit_scale, bias, out):
             neg_max[j] = columns.tile([P, 1], F32, name="neg_max")
             nc.vector.tensor_reduce(out=neg_max[j][:], in_=neg_s[j][:, :N], axis=AXIS.X, op=ALU.min)
 
+        def of_tile(pairs, j):
+            if j // 2 not in pairs:
+                pairs[j // 2] = columns.tile([P, 2], F32, name="sums")
+            return pairs[j // 2][:, j % 2 : j % 2 + 1]
+
         def exponential(j):
             e_bf[j] = work.tile([P, N], BF16, name="e_bf")
-            row_sum[j] = columns.tile([P, 1], F32, name="row_sum")
             nc.scalar.activation(
                 out=e_bf[j][:].rearrange("q (b p e) -> q b p e", p=P, e=2),
                 in_=neg_s[j][:, :N].rearrange("q (b e p) -> q b p e", p=P, e=2),
                 func=ACT.Exp,
                 bias=neg_max[j][:],
                 scale=-1.0,
-                accum_out=row_sum[j][:],
+                accum_out=of_tile(row_sums, j),
             )
 
         def transpose_e(j):
@@ -244,9 +253,12 @@ def tile_attention_pa_t_kernel(tc, q_hat, k_hat, v, logit_scale, bias, out):
                 in_=e_grouped[j][:].rearrange("p g q t -> p (g q t)"),
             )
 
+        def invert_two_sums(j):
+            inv_sums[j // 2] = columns.tile([P, 2], F32, name="inv_sums")
+            nc.vector.reciprocal(out=inv_sums[j // 2][:], in_=row_sums[j // 2][:])
+
         def invert_sum(j):
-            inv_sum[j] = columns.tile([P, 1], F32, name="inv_sum")
-            nc.vector.reciprocal(out=inv_sum[j][:], in_=row_sum[j][:])
+            nc.vector.reciprocal(out=of_tile(inv_sums, j), in_=of_tile(row_sums, j))
 
         def mx_passes(j):
             head = j // TILES
@@ -282,7 +294,7 @@ def tile_attention_pa_t_kernel(tc, q_hat, k_hat, v, logit_scale, bias, out):
 
         def output(j, on_vector=False):
             x_sb = work.tile([P, D], F32, name="x_sb")
-            normalise(x_sb[:], x_bank[j][:], inv_sum[j][:], on_vector)
+            normalise(x_sb[:], x_bank[j][:], of_tile(inv_sums, j), on_vector)
             store(j, x_sb, slice(0, D))
 
         half_sum, half_e, half_bank, half_grouped, half_words, half_scales, half_x_bank = {}, {}, {}, {}, {}, {}, {}
@@ -329,8 +341,7 @@ def tile_attention_pa_t_kernel(tc, q_hat, k_hat, v, logit_scale, bias, out):
             nc.vector.quantize_mx(out=half_words[g][:].bitcast(FP8X4), scales=half_scales[g][:], in_=half_grouped[g][:])
 
         def join_sum(j):
-            row_sum[j] = columns.tile([P, 1], F32, name="row_sum")
-            nc.vector.tensor_reduce(out=row_sum[j][:], in_=half_sum[j][:], axis=AXIS.X, op=ALU.add)
+            nc.vector.tensor_reduce(out=of_tile(row_sums, j), in_=half_sum[j][:], axis=AXIS.X, op=ALU.add)
 
         def mx_pass_by_halves(j, g, words, scales):
             head = j // TILES
@@ -351,7 +362,7 @@ def tile_attention_pa_t_kernel(tc, q_hat, k_hat, v, logit_scale, bias, out):
         def output_by_halves(j):
             for half, queue in enumerate((nc.sync, nc.scalar)):
                 x_sb = work.tile([P, D // 2], F32, name="half_x_sb")
-                normalise(x_sb[:], half_x_bank[(j, half)][:, : D // 2], inv_sum[j][:], on_vector=(half == 0))
+                normalise(x_sb[:], half_x_bank[(j, half)][:, : D // 2], of_tile(inv_sums, j), on_vector=(half == 0))
                 store(j, x_sb, slice(half * D // 2, (half + 1) * D // 2), queue)
 
         zeros = const.tile([P, BANK], BF16, name="zeros")
@@ -366,8 +377,9 @@ def tile_attention_pa_t_kernel(tc, q_hat, k_hat, v, logit_scale, bias, out):
         make_identity(nc, identity_f32[:])
         bias_sb = [const.tile([P, TILES, N], BF16, name="bias%d" % h) for h in range(NHEADS)]
         new_head(0)
-        load_keys(k_raw[0], k_rows, first_row(0), 0, 4)
+        load_first_keys(k_raw[0], k_rows, first_row(0), 0, 2)
         load_blocks(q_raw[0], q_rows, first_row(0), 0, 1)
+        load_first_keys(k_raw[0], k_rows, first_row(0), 2, 2)
         load_keys(k_raw[0], k_rows, first_row(0), 4, 4)
         log_factor = const.tile([P, NHEADS], BF16, name="log_factor")
         nc.sync.dma_start(out=log_factor[:], in_=logit_scale.rearrange("h a b -> (h a b)").partition_broadcast(P))
@@ -383,13 +395,23 @@ def tile_attention_pa_t_kernel(tc, q_hat, k_hat, v, logit_scale, bias, out):
         nc.scalar.activation(out=unread[:], in_=zeros[:, :1], func=ACT.Exp)
 
         warm_up(WARM_UP)
-        unit_transposes(0, 0)
-        unit_copy(0, 0, on_vector=True)
-        unit_transposes(0, 1)
-        unit_copy(0, 1, on_vector=False)
-        unit_transposes(0, 4, members=range(2), in_output_bank=True)
+        for members in (range(2), range(2, 4)):
+            for unit in range(2):
+                unit_transposes(0, unit, members)
+            if members[0] == 0:
+                unit_transposes(0, 4, members, in_output_bank=True)
         unit_copy(0, 4, on_vector=True, members=range(2))
+        unit_copy(0, 0, on_vector=False)
+        unit_copy(0, 1, on_vector=True)
         warm_up(2)
+
+        factor = const.tile([P, NHEADS], F32, name="factor")
+        nc.scalar.activation(out=factor[:], in_=log_factor[:], func=ACT.Exp)
+        neg_factor = const.tile([P, NHEADS], F32, name="neg_factor")
+        nc.vector.tensor_scalar(
+            out=neg_factor[:], in0=factor[:], scalar1=100.0, scalar2=-1.0, op0=ALU.min, op1=ALU.mult
+        )
+
         scores(0, 0, chunks=range(2))
         unit_transposes(0, 2, in_output_bank=True)
         unit_copy(0, 2, on_vector=False)
@@ -399,12 +421,6 @@ def tile_attention_pa_t_kernel(tc, q_hat, k_hat, v, logit_scale, bias, out):
         unit_transposes(0, 4, members=range(2, 4))
         unit_copy(0, 4, on_vector=False, members=range(2, 4))
 
-        factor = const.tile([P, NHEADS], F32, name="factor")
-        nc.scalar.activation(out=factor[:], in_=log_factor[:], func=ACT.Exp)
-        neg_factor = const.tile([P, NHEADS], F32, name="neg_factor")
-        nc.vector.tensor_scalar(
-            out=neg_factor[:], in0=factor[:], scalar1=100.0, scalar2=-1.0, op0=ALU.min, op1=ALU.mult
-        )
         for piece in range(V_PIECES):
             regroup_v(0, piece)
 
@@ -428,14 +444,11 @@ def tile_attention_pa_t_kernel(tc, q_hat, k_hat, v, logit_scale, bias, out):
                 load_blocks(bias_sb[1], bias_rows, N, 0, TILES)
 
             unit = None
-            first = FIRST_UNIT_STEP[head]
-            if i < len(UNITS_IN_A_HEAD[head]):
-                unit_head, unit = head, UNITS_IN_A_HEAD[head][i]
-            elif preparing and first <= i < first + len(UNITS_BEFORE_A_HEAD):
-                unit_head, unit = prepare, UNITS_BEFORE_A_HEAD[i - first]
+            if step < len(FIRST_HEAD_UNITS):
+                unit_head, unit = head, FIRST_HEAD_UNITS[step]
+            elif preparing and i >= FIRST_UNIT_STEP:
+                unit_head, unit = prepare, UNITS_BEFORE_A_HEAD[i - FIRST_UNIT_STEP]
             has_unit = unit is not None
-
-            turn_head, turn = divmod(step + TILES - FIRST_TURN_STEP, TILES)
 
             if step > 0:
                 scores(step, 0)
@@ -453,20 +466,22 @@ def tile_attention_pa_t_kernel(tc, q_hat, k_hat, v, logit_scale, bias, out):
             if step == LAST:
                 first_half_maximum(step)
             add_bias(step, 1)
+            turn_head, turn_step = divmod(step + TILES - FIRST_TURN_STEP, TILES)
             if 0 < turn_head < len(HEADS):
-                turn_queries(turn_head, turn)
-            if is_tile(step - QUANTISE_LAG):
-                invert_sum(step - QUANTISE_LAG)
+                first_turn = sum(TURNS_OF_STEP[:turn_step])
+                for turn in range(first_turn, first_turn + TURNS_OF_STEP[turn_step]):
+                    turn_queries(turn_head, turn)
+            if is_tile(step - QUANTISE_LAG) and (step - QUANTISE_LAG) % 2 == 0:
+                invert_two_sums(step - QUANTISE_LAG)
             if step == LAST:
                 second_half_maximum(step)
             else:
                 row_maximum(step)
             if step == MX_LAG - 2:
-                for part in range(V_PARTS):
-                    quantise_v(0, part)
+                quantise_v(0, 0, V_PARTS)
             v_head, part = divmod(step + TILES - V_FIRST_STEP - 1, TILES)
             if 0 < v_head < len(HEADS) and part < V_PARTS:
-                quantise_v(v_head, part)
+                quantise_v(v_head, part, 1)
 
             if is_tile(step - EXP_LAG):
                 exponential(step - EXP_LAG)
@@ -490,7 +505,6 @@ def tile_attention_pa_t_kernel(tc, q_hat, k_hat, v, logit_scale, bias, out):
         quantise_e(LAST - 2)
         mx_passes(LAST - 2)
         quantise_e(LAST - 1)
-        invert_sum(LAST - 2)
         invert_sum(LAST - 1)
         output(LAST - 3, on_vector=True)
         output(LAST - 2, on_vector=False)

@@ -30,17 +30,18 @@ LAST = ALL_TILES - 1
 FIRST_LATE_TILE = ALL_TILES - MX_LAG
 
 UNITS_BEFORE_A_HEAD = (0, 1, 4, 2, 3)
-FIRST_HEAD_UNITS = (5, 6, 7)
 FIRST_UNIT_STEP = TILES - len(UNITS_BEFORE_A_HEAD)
 BLOCK = 32
-TURNED = 2
-FIRST_TURN_STEP = 4
-TURNS_OF_STEP = (2, 2, 1, 1, 1, 1, 2, 2)
+TURNED_FROM = (8, 8, 2, 2)
+LOAD_STEPS = (None, 0, 6, 14)
+FIRST_TURN_STEP = 3
+TURNS_OF_STEP = (3, 3, 3, 3)
 
 V_PIECES = 8
 V_PARTS = 4
+SCALAR_PIECES = 2
 V_PIECES_A_PART = V_PIECES // V_PARTS
-V_FIRST_STEP = 5
+V_FIRST_STEP = 7
 
 WARM_UP = 4
 
@@ -96,8 +97,8 @@ def tile_attention_pa_t_kernel(tc, q_hat, k_hat, v, logit_scale, bias, out):
             )
 
         def load_queries(head):
-            rows = slice(first_row(head) + TURNED * P, first_row(head) + N)
-            q_blocks[head] = raw.tile([P, 2, (N - TURNED * P) // BLOCK, 2 * BLOCK], BF16, name="q_blocks", align_bytes=64)
+            rows = slice(first_row(head) + TURNED_FROM[head] * P, first_row(head) + N)
+            q_blocks[head] = raw.tile([P, 2, (N - TURNED_FROM[head] * P) // BLOCK, 2 * BLOCK], BF16, name="q_blocks", align_bytes=64)
             for u in range(2):
                 for quadrant in range(P // BLOCK):
                     column = 2 * (u * P + quadrant * BLOCK)
@@ -106,10 +107,12 @@ def tile_attention_pa_t_kernel(tc, q_hat, k_hat, v, logit_scale, bias, out):
                         in_=q_rows[rows, column : column + 2 * BLOCK].rearrange("(b r) c -> r b c", r=BLOCK),
                     )
 
-        def new_head(head):
+        def new_raw(head):
             q_raw[head] = raw.tile([P, TILES, D], BF16, name="q_raw")
             k_raw[head] = raw.tile([P, TILES, D], BF16, name="k_raw")
             v_raw[head] = raw.tile([P, TILES, D], BF16, name="v_raw")
+
+        def new_operands(head):
             q_t[head] = operands.tile([P, TILES, 2, P], F32, name="q_t", align_bytes=64)
             k_t[head] = operands.tile([P, 2, N], F32, name="k_t")
 
@@ -145,27 +148,23 @@ def tile_attention_pa_t_kernel(tc, q_hat, k_hat, v, logit_scale, bias, out):
             tile_turned, u = divmod(turn, 2)
             blocks = P // BLOCK
             nc.vector.transpose(
-                q_t[head][:, TURNED + tile_turned, u, :],
+                q_t[head][:, TURNED_FROM[head] + tile_turned, u, :],
                 q_blocks[head][:, u, tile_turned * blocks : (tile_turned + 1) * blocks, :]
                 .rearrange("p b c -> p (b c)")
                 .bitcast(F32),
             )
 
-        def regroup_v(head, piece):
+        def regroup_v(head, piece, on_scalar=False):
             if piece == 0:
                 v_grouped[head] = operands.tile([P, PASSES, D, PACK], BF16, name="v_grouped", bufs=1, align_bytes=64)
             g, part = divmod(piece, V_PIECES // PASSES)
             width = D * PASSES // V_PIECES
-            nc.gpsimd.tensor_scalar(
-                out=v_grouped[head][:, g, part * width : (part + 1) * width, :],
-                in0=v_raw[head][:, PACK * g : PACK * (g + 1), part * width : (part + 1) * width].rearrange(
-                    "p t d -> p d t"
-                ),
-                scalar1=1.0,
-                scalar2=0.0,
-                op0=ALU.mult,
-                op1=ALU.add,
-            )
+            dst = v_grouped[head][:, g, part * width : (part + 1) * width, :]
+            src = v_raw[head][:, PACK * g : PACK * (g + 1), part * width : (part + 1) * width].rearrange("p t d -> p d t")
+            if on_scalar:
+                nc.scalar.copy(out=dst, in_=src)
+            else:
+                nc.gpsimd.tensor_scalar(out=dst, in0=src, scalar1=1.0, scalar2=0.0, op0=ALU.mult, op1=ALU.add)
 
         def quantise_v(head, first_part, count):
             if first_part == 0:
@@ -376,7 +375,8 @@ def tile_attention_pa_t_kernel(tc, q_hat, k_hat, v, logit_scale, bias, out):
         identity_f32 = const.tile([P, P], F32, name="identity_f32")
         make_identity(nc, identity_f32[:])
         bias_sb = [const.tile([P, TILES, N], BF16, name="bias%d" % h) for h in range(NHEADS)]
-        new_head(0)
+        new_raw(0)
+        new_operands(0)
         load_first_keys(k_raw[0], k_rows, first_row(0), 0, 2)
         load_blocks(q_raw[0], q_rows, first_row(0), 0, 1)
         load_first_keys(k_raw[0], k_rows, first_row(0), 2, 2)
@@ -421,7 +421,7 @@ def tile_attention_pa_t_kernel(tc, q_hat, k_hat, v, logit_scale, bias, out):
         unit_transposes(0, 4, members=range(2, 4))
         unit_copy(0, 4, on_vector=False, members=range(2, 4))
 
-        for piece in range(V_PIECES):
+        for piece in range(V_PIECES - SCALAR_PIECES):
             regroup_v(0, piece)
 
         def is_tile(j):
@@ -433,28 +433,35 @@ def tile_attention_pa_t_kernel(tc, q_hat, k_hat, v, logit_scale, bias, out):
             preparing = prepare < len(HEADS)
 
             if preparing and i == 0:
-                new_head(prepare)
-                load_keys(k_raw[prepare], k_rows, first_row(prepare), 0, TILES)
-            if preparing and i == 1:
-                load_blocks(q_raw[prepare], q_rows, first_row(prepare), 0, TURNED)
-                load_queries(prepare)
-            if preparing and i == 2:
-                load_keys(v_raw[prepare], v_rows, first_row(prepare), 0, TILES)
-            if step == 3:
-                load_blocks(bias_sb[1], bias_rows, N, 0, TILES)
+                new_operands(prepare)
+            for loaded in range(1, len(HEADS)):
+                load_step = step - LOAD_STEPS[loaded]
+                if load_step == 0:
+                    new_raw(loaded)
+                    load_keys(k_raw[loaded], k_rows, first_row(loaded), 0, TILES)
+                if load_step == 1:
+                    load_blocks(q_raw[loaded], q_rows, first_row(loaded), 0, TURNED_FROM[loaded])
+                    if TURNED_FROM[loaded] < TILES:
+                        load_queries(loaded)
+                if load_step == 2:
+                    load_keys(v_raw[loaded], v_rows, first_row(loaded), 0, TILES)
+            if step in (3, 4):
+                load_blocks(bias_sb[1], bias_rows, N, 4 * (step - 3), 4)
 
             unit = None
-            if step < len(FIRST_HEAD_UNITS):
-                unit_head, unit = head, FIRST_HEAD_UNITS[step]
+            if 5 + i < 4 + TURNED_FROM[head] // 2:
+                unit_head, unit = head, 5 + i
             elif preparing and i >= FIRST_UNIT_STEP:
                 unit_head, unit = prepare, UNITS_BEFORE_A_HEAD[i - FIRST_UNIT_STEP]
             has_unit = unit is not None
 
             if step > 0:
                 scores(step, 0)
-            if is_tile(step - MX_LAG):
+            if step > MX_LAG:
                 mx_passes(step - MX_LAG)
             scores(step, 1)
+            if step == MX_LAG:
+                mx_passes(0)
             if is_tile(step - TRANSPOSE_LAG):
                 transpose_e(step - TRANSPOSE_LAG)
             if has_unit:
@@ -463,11 +470,14 @@ def tile_attention_pa_t_kernel(tc, q_hat, k_hat, v, logit_scale, bias, out):
             add_bias(step, 0)
             if is_tile(step - QUANTISE_LAG):
                 quantise_e(step - QUANTISE_LAG)
+            v_head, part = divmod(step + TILES - V_FIRST_STEP - 1, TILES)
+            if 0 < v_head < len(HEADS) and part < V_PARTS:
+                quantise_v(v_head, part, 1)
             if step == LAST:
                 first_half_maximum(step)
             add_bias(step, 1)
             turn_head, turn_step = divmod(step + TILES - FIRST_TURN_STEP, TILES)
-            if 0 < turn_head < len(HEADS):
+            if turn_head < len(HEADS) and TURNED_FROM[turn_head] < TILES and turn_step < len(TURNS_OF_STEP):
                 first_turn = sum(TURNS_OF_STEP[:turn_step])
                 for turn in range(first_turn, first_turn + TURNS_OF_STEP[turn_step]):
                     turn_queries(turn_head, turn)
@@ -479,9 +489,6 @@ def tile_attention_pa_t_kernel(tc, q_hat, k_hat, v, logit_scale, bias, out):
                 row_maximum(step)
             if step == MX_LAG - 2:
                 quantise_v(0, 0, V_PARTS)
-            v_head, part = divmod(step + TILES - V_FIRST_STEP - 1, TILES)
-            if 0 < v_head < len(HEADS) and part < V_PARTS:
-                quantise_v(v_head, part, 1)
 
             if is_tile(step - EXP_LAG):
                 exponential(step - EXP_LAG)
@@ -492,8 +499,13 @@ def tile_attention_pa_t_kernel(tc, q_hat, k_hat, v, logit_scale, bias, out):
             if has_unit:
                 unit_copy(unit_head, unit, on_vector=False)
 
+            if step < SCALAR_PIECES:
+                regroup_v(0, V_PIECES - 1 - step, on_scalar=True)
+
             v_head, part = divmod(step + TILES - V_FIRST_STEP, TILES)
             if 0 < v_head < len(HEADS) and part < V_PARTS:
+                unread_word = columns.tile([P, 1], U32, name="unread_word")
+                nc.gpsimd.tensor_copy(out=unread_word[:], in_=e_words[step - QUANTISE_LAG][:, :1])
                 for piece in range(part * V_PIECES_A_PART, (part + 1) * V_PIECES_A_PART):
                     regroup_v(v_head, piece)
 

@@ -29,21 +29,23 @@ MX_LAG = 4
 LAST = ALL_TILES - 1
 FIRST_LATE_TILE = ALL_TILES - MX_LAG
 
-UNITS_BEFORE_A_HEAD = (0, 1, 4, 2, 3)
-FIRST_UNIT_STEP = TILES - len(UNITS_BEFORE_A_HEAD)
+UNIT_STEPS = ((), (3, 3, 4, 5, 6), (2, 3, 4, 5, 6), (2, 3, 4, 5, 6))
+OWN_UNIT_STEPS = (0, 2, 3)
+TURNED_FROM = (8, 4, 2, 2)
+FIRST_TURN_STEP = (None, 4, 3, 3)
+TURNS_A_STEP = 3
 BLOCK = 32
-TURNED_FROM = (8, 8, 2, 2)
-LOAD_STEPS = (None, 0, 6, 14)
-FIRST_TURN_STEP = 3
-TURNS_OF_STEP = (3, 3, 3, 3)
 
+LOAD_STEP = (None, -1, 6, 14)
+
+V_FIRST_STEP = 7
 V_PIECES = 8
 V_PARTS = 4
-SCALAR_PIECES = 2
 V_PIECES_A_PART = V_PIECES // V_PARTS
-V_FIRST_STEP = 7
+SCALAR_PIECES = 2
 
-WARM_UP = 4
+WARM_UP = 5
+WARM_UP_AGAIN = 2
 
 
 def tile_attention_pa_t_kernel(tc, q_hat, k_hat, v, logit_scale, bias, out):
@@ -96,9 +98,10 @@ def tile_attention_pa_t_kernel(tc, q_hat, k_hat, v, logit_scale, bias, out):
                 in_=rows[row0 + first * P : row0 + (first + count) * P, :].rearrange("(t p) d -> p t d", p=P),
             )
 
-        def load_queries(head):
-            rows = slice(first_row(head) + TURNED_FROM[head] * P, first_row(head) + N)
-            q_blocks[head] = raw.tile([P, 2, (N - TURNED_FROM[head] * P) // BLOCK, 2 * BLOCK], BF16, name="q_blocks", align_bytes=64)
+        def load_queries_to_turn(head):
+            first = TURNED_FROM[head] * P
+            rows = slice(first_row(head) + first, first_row(head) + N)
+            q_blocks[head] = raw.tile([P, 2, (N - first) // BLOCK, 2 * BLOCK], BF16, name="q_blocks", align_bytes=64)
             for u in range(2):
                 for quadrant in range(P // BLOCK):
                     column = 2 * (u * P + quadrant * BLOCK)
@@ -134,7 +137,8 @@ def tile_attention_pa_t_kernel(tc, q_hat, k_hat, v, logit_scale, bias, out):
         def unit_copy(head, unit, on_vector, members=range(4)):
             if unit < 4:
                 key_half, u = divmod(unit, 2)
-                dst = k_t[head][:, u, key_half * BANK : (key_half + 1) * BANK]
+                first = key_half * BANK
+                dst = k_t[head][:, u, first + members[0] * P : first + (members[-1] + 1) * P]
             else:
                 tiles = slice(2 * (unit - 4) + members[0] // 2, 2 * (unit - 4) + (members[-1] + 1) // 2)
                 dst = q_t[head][:, tiles, :, :].rearrange("p i u q -> p (i u q)")
@@ -325,14 +329,12 @@ def tile_attention_pa_t_kernel(tc, q_hat, k_hat, v, logit_scale, bias, out):
                     half_bank[g][:, u, :], half_e[g][:, 2 * u * P : 2 * (u + 1) * P].bitcast(F32), identity_f32[:]
                 )
 
-        def half_regroup(g, on_vector):
+        def half_regroup(g):
             half_grouped[g] = work.tile([P, P * PACK], BF16, name="half_grouped", align_bytes=64)
-            dst = half_grouped[g][:].bitcast(F32).rearrange("p (q u) -> p q u", u=2)
-            src = half_bank[g][:].rearrange("p u q -> p q u")
-            if on_vector:
-                nc.vector.tensor_copy(out=dst, in_=src)
-            else:
-                nc.scalar.copy(out=dst, in_=src)
+            nc.scalar.copy(
+                out=half_grouped[g][:].bitcast(F32).rearrange("p (q u) -> p q u", u=2),
+                in_=half_bank[g][:].rearrange("p u q -> p q u"),
+            )
 
         def half_quantise(g):
             half_words[g] = work.tile([P, P], U32, name="half_words", align_bytes=64)
@@ -389,7 +391,9 @@ def tile_attention_pa_t_kernel(tc, q_hat, k_hat, v, logit_scale, bias, out):
         load_blocks(bias_sb[0], bias_rows, 0, 1, 1)
         load_blocks(q_raw[0], q_rows, first_row(0), 4, 4)
         load_blocks(bias_sb[0], bias_rows, 0, 2, 2)
-        load_blocks(bias_sb[0], bias_rows, 0, 4, 4)
+        new_raw(1)
+        load_keys(k_raw[1], k_rows, first_row(1), 0, TILES)
+        load_blocks(bias_sb[0], bias_rows, 0, 4, 2)
 
         unread = const.tile([P, 1], F32, name="unread")
         nc.scalar.activation(out=unread[:], in_=zeros[:, :1], func=ACT.Exp)
@@ -398,12 +402,11 @@ def tile_attention_pa_t_kernel(tc, q_hat, k_hat, v, logit_scale, bias, out):
         for members in (range(2), range(2, 4)):
             for unit in range(2):
                 unit_transposes(0, unit, members)
+                unit_copy(0, unit, on_vector=(unit == 1), members=members)
             if members[0] == 0:
                 unit_transposes(0, 4, members, in_output_bank=True)
-        unit_copy(0, 4, on_vector=True, members=range(2))
-        unit_copy(0, 0, on_vector=False)
-        unit_copy(0, 1, on_vector=True)
-        warm_up(2)
+                unit_copy(0, 4, on_vector=True, members=members)
+        warm_up(WARM_UP_AGAIN)
 
         factor = const.tile([P, NHEADS], F32, name="factor")
         nc.scalar.activation(out=factor[:], in_=log_factor[:], func=ACT.Exp)
@@ -432,28 +435,27 @@ def tile_attention_pa_t_kernel(tc, q_hat, k_hat, v, logit_scale, bias, out):
             prepare = head + 1
             preparing = prepare < len(HEADS)
 
-            if preparing and i == 0:
-                new_operands(prepare)
             for loaded in range(1, len(HEADS)):
-                load_step = step - LOAD_STEPS[loaded]
-                if load_step == 0:
+                if step == LOAD_STEP[loaded]:
                     new_raw(loaded)
                     load_keys(k_raw[loaded], k_rows, first_row(loaded), 0, TILES)
-                if load_step == 1:
+                if step == LOAD_STEP[loaded] + 1:
                     load_blocks(q_raw[loaded], q_rows, first_row(loaded), 0, TURNED_FROM[loaded])
-                    if TURNED_FROM[loaded] < TILES:
-                        load_queries(loaded)
-                if load_step == 2:
+                    load_queries_to_turn(loaded)
+                if step == LOAD_STEP[loaded] + 2:
                     load_keys(v_raw[loaded], v_rows, first_row(loaded), 0, TILES)
+            if step == 2:
+                load_blocks(bias_sb[0], bias_rows, 0, 6, 2)
             if step in (3, 4):
                 load_blocks(bias_sb[1], bias_rows, N, 4 * (step - 3), 4)
 
-            unit = None
-            if 5 + i < 4 + TURNED_FROM[head] // 2:
-                unit_head, unit = head, 5 + i
-            elif preparing and i >= FIRST_UNIT_STEP:
-                unit_head, unit = prepare, UNITS_BEFORE_A_HEAD[i - FIRST_UNIT_STEP]
-            has_unit = unit is not None
+            if preparing and i == 0:
+                new_operands(prepare)
+            units = []
+            if i in OWN_UNIT_STEPS and 2 * OWN_UNIT_STEPS.index(i) + 2 < TURNED_FROM[head]:
+                units.append((head, 5 + OWN_UNIT_STEPS.index(i)))
+            if preparing:
+                units.extend((prepare, unit) for unit, unit_step in enumerate(UNIT_STEPS[prepare]) if unit_step == i)
 
             if step > 0:
                 scores(step, 0)
@@ -464,8 +466,8 @@ def tile_attention_pa_t_kernel(tc, q_hat, k_hat, v, logit_scale, bias, out):
                 mx_passes(0)
             if is_tile(step - TRANSPOSE_LAG):
                 transpose_e(step - TRANSPOSE_LAG)
-            if has_unit:
-                unit_transposes(unit_head, unit)
+            for count, (unit_head, unit) in enumerate(units):
+                unit_transposes(unit_head, unit, in_output_bank=(count > 0))
 
             add_bias(step, 0)
             if is_tile(step - QUANTISE_LAG):
@@ -476,11 +478,11 @@ def tile_attention_pa_t_kernel(tc, q_hat, k_hat, v, logit_scale, bias, out):
             if step == LAST:
                 first_half_maximum(step)
             add_bias(step, 1)
-            turn_head, turn_step = divmod(step + TILES - FIRST_TURN_STEP, TILES)
-            if turn_head < len(HEADS) and TURNED_FROM[turn_head] < TILES and turn_step < len(TURNS_OF_STEP):
-                first_turn = sum(TURNS_OF_STEP[:turn_step])
-                for turn in range(first_turn, first_turn + TURNS_OF_STEP[turn_step]):
-                    turn_queries(turn_head, turn)
+            if preparing:
+                first_turn = (i - FIRST_TURN_STEP[prepare]) * TURNS_A_STEP
+                turns = 2 * (TILES - TURNED_FROM[prepare])
+                for turn in range(max(first_turn, 0), min(first_turn + TURNS_A_STEP, turns)):
+                    turn_queries(prepare, turn)
             if is_tile(step - QUANTISE_LAG) and (step - QUANTISE_LAG) % 2 == 0:
                 invert_two_sums(step - QUANTISE_LAG)
             if step == LAST:
@@ -496,9 +498,8 @@ def tile_attention_pa_t_kernel(tc, q_hat, k_hat, v, logit_scale, bias, out):
                 output(step - MX_LAG)
             if is_tile(step - TRANSPOSE_LAG):
                 regroup_e(step - TRANSPOSE_LAG)
-            if has_unit:
+            for unit_head, unit in units:
                 unit_copy(unit_head, unit, on_vector=False)
-
             if step < SCALAR_PIECES:
                 regroup_v(0, V_PIECES - 1 - step, on_scalar=True)
 
@@ -519,16 +520,16 @@ def tile_attention_pa_t_kernel(tc, q_hat, k_hat, v, logit_scale, bias, out):
         quantise_e(LAST - 1)
         invert_sum(LAST - 1)
         output(LAST - 3, on_vector=True)
-        output(LAST - 2, on_vector=False)
         half_transpose(0)
         half_transpose(1)
         for g in range(PASSES):
             queries = slice(g * P, (g + 1) * P)
             mx_pass_by_halves(LAST - 1, g, e_words[LAST - 1][:, queries], e_scales[LAST - 1][:, queries])
         join_sum(LAST)
-        half_regroup(0, on_vector=True)
+        output(LAST - 2, on_vector=True)
+        half_regroup(0)
         half_quantise(0)
-        half_regroup(1, on_vector=False)
+        half_regroup(1)
         half_quantise(1)
         for g in range(PASSES):
             mx_pass_by_halves(LAST, g, half_words[g][:], half_scales[g][:])

from contextlib import ExitStack

import concourse.mybir as mybir
from concourse.masks import make_identity

F32 = mybir.dt.float32
BF16 = mybir.dt.bfloat16
U32 = mybir.dt.uint32
U8 = mybir.dt.uint8
FP8X4 = mybir.dt.float8_e4m3fn_x4
ALU = mybir.AluOpType
ACT = mybir.ActivationFunctionType
AXIS = mybir.AxisListType

WINDOWS, NHEADS, N, D = 2, 2, 1024, 512
P = 128
TILES = N // P
BANK = 512
PACK = 4
PASSES = N // (P * PACK)
HEADS = [(0, 0), (1, 0), (0, 1), (1, 1)]
ALL_TILES = len(HEADS) * TILES
FLOPS = 2 * 2 * WINDOWS * NHEADS * N * N * D

EXP_LAG = 1
TRANSPOSE_LAG = 2
QUANTISE_LAG = 3
MX_LAG = 4
LAST = ALL_TILES - 1
FIRST_LATE_TILE = ALL_TILES - MX_LAG

UNIT_STEPS = ((), (3, 3, 4, 5, 6), (2, 3, 4, 5, 6), (2, 3, 4, 5, 6))
OWN_UNIT_STEPS = (0, 2, 3)
TURNED_FROM = (8, 4, 2, 2)
FIRST_TURN_STEP = (None, 4, 3, 3)
TURNS_A_STEP = 3
BLOCK = 32

LOAD_STEP = (None, -1, 6, 14)

V_FIRST_STEP = 7
V_PIECES = 8
V_PARTS = 4
V_PIECES_A_PART = V_PIECES // V_PARTS
SCALAR_PIECES = 2

WARM_UP = 5
WARM_UP_AGAIN = 2


def tile_attention_pa_t_kernel(tc, q_hat, k_hat, v, logit_scale, bias, out):
    nc = tc.nc
    q_rows = q_hat.rearrange("b h n d -> (b h n) d")
    k_rows = k_hat.rearrange("b h n d -> (b h n) d")
    v_rows = v.rearrange("b h n d -> (b h n) d")
    bias_rows = bias.rearrange("h q k -> (h q) k")
    out_rows = out.rearrange("b x (n h d) -> (b x n) h d", h=NHEADS, d=D)

    with ExitStack() as ctx:
        const = ctx.enter_context(tc.tile_pool(name="const", bufs=1))
        raw = ctx.enter_context(tc.tile_pool(name="raw", bufs=2))
        operands = ctx.enter_context(tc.tile_pool(name="operands", bufs=2))
        work = ctx.enter_context(tc.tile_pool(name="work", bufs=4))
        columns = ctx.enter_context(tc.tile_pool(name="columns", bufs=8))
        score_banks = ctx.enter_context(tc.psum_pool(name="score_banks", bufs=4))
        transpose_banks = ctx.enter_context(tc.psum_pool(name="transpose_banks", bufs=2))
        output_banks = ctx.enter_context(tc.psum_pool(name="output_banks", bufs=2))
        ctx.enter_context(tc.manual_schedule())

        q_raw, q_blocks, k_raw, v_raw, q_t, k_t, v_grouped, v_words, v_scales, unit_bank = (
            {}, {}, {}, {}, {}, {}, {}, {}, {}, {},
        )
        score, neg_s, neg_max, row_sums, inv_sums, e_bf, e_bank, e_grouped, e_words, e_scales, x_bank = (
            {}, {}, {}, {}, {}, {}, {}, {}, {}, {}, {},
        )

        def first_row(head):
            b, h = HEADS[head]
            return (b * NHEADS + h) * N

        def load_keys(dst, rows, row0, first, count):
            nc.sync.dma_start(
                out=dst[:, first : first + count, :].rearrange("p (g t) d -> p g t d", t=PACK),
                in_=rows[row0 + first * P : row0 + (first + count) * P, :].rearrange(
                    "(g p t) d -> p g t d", p=P, t=PACK
                ),
            )

        def load_first_keys(dst, rows, row0, t0, count):
            nc.sync.dma_start(
                out=dst[:, t0 : t0 + count, :],
                in_=rows[row0 : row0 + PACK * P, :].rearrange("(p t) d -> p t d", t=PACK)[:, t0 : t0 + count, :],
            )

        def load_blocks(dst, rows, row0, first, count):
            nc.sync.dma_start(
                out=dst[:, first : first + count, :],
                in_=rows[row0 + first * P : row0 + (first + count) * P, :].rearrange("(t p) d -> p t d", p=P),
            )

        def load_queries_to_turn(head):
            first = TURNED_FROM[head] * P
            rows = slice(first_row(head) + first, first_row(head) + N)
            q_blocks[head] = raw.tile([P, 2, (N - first) // BLOCK, 2 * BLOCK], BF16, name="q_blocks", align_bytes=64)
            for u in range(2):
                for quadrant in range(P // BLOCK):
                    column = 2 * (u * P + quadrant * BLOCK)
                    nc.sync.dma_start(
                        out=q_blocks[head][quadrant * BLOCK : (quadrant + 1) * BLOCK, u, :, :],
                        in_=q_rows[rows, column : column + 2 * BLOCK].rearrange("(b r) c -> r b c", r=BLOCK),
                    )

        def new_raw(head):
            q_raw[head] = raw.tile([P, TILES, D], BF16, name="q_raw")
            k_raw[head] = raw.tile([P, TILES, D], BF16, name="k_raw")
            v_raw[head] = raw.tile([P, TILES, D], BF16, name="v_raw")

        def new_operands(head):
            q_t[head] = operands.tile([P, TILES, 2, P], F32, name="q_t", align_bytes=64)
            k_t[head] = operands.tile([P, 2, N], F32, name="k_t")

        def unit_transposes(head, unit, members=range(4), in_output_bank=False):
            if members[0] == 0 and in_output_bank:
                unit_bank[(head, unit)] = output_banks.tile([P, 4, P], F32, name="early_unit_bank", tag="x_bank")
            elif members[0] == 0:
                unit_bank[(head, unit)] = transpose_banks.tile([P, 4, P], F32, name="unit_bank", tag="bank")
            bank = unit_bank[(head, unit)]
            for m in members:
                if unit < 4:
                    key_half, u = divmod(unit, 2)
                    src = k_raw[head][:, 4 * key_half + m, 2 * u * P : 2 * (u + 1) * P]
                else:
                    tile_in_pair, u = divmod(m, 2)
                    src = q_raw[head][:, 2 * (unit - 4) + tile_in_pair, 2 * u * P : 2 * (u + 1) * P]
                nc.tensor.transpose(bank[:, m, :], src.bitcast(F32), identity_f32[:])

        def unit_copy(head, unit, on_vector, members=range(4)):
            if unit < 4:
                key_half, u = divmod(unit, 2)
                first = key_half * BANK
                dst = k_t[head][:, u, first + members[0] * P : first + (members[-1] + 1) * P]
            else:
                tiles = slice(2 * (unit - 4) + members[0] // 2, 2 * (unit - 4) + (members[-1] + 1) // 2)
                dst = q_t[head][:, tiles, :, :].rearrange("p i u q -> p (i u q)")
            src = unit_bank[(head, unit)][:, members[0] : members[-1] + 1, :].rearrange("p m c -> p (m c)")
            if on_vector:
                nc.vector.tensor_copy(out=dst, in_=src)
            else:
                nc.scalar.copy(out=dst, in_=src)

        def turn_queries(head, turn):
            tile_turned, u = divmod(turn, 2)
            blocks = P // BLOCK
            nc.vector.transpose(
                q_t[head][:, TURNED_FROM[head] + tile_turned, u, :],
                q_blocks[head][:, u, tile_turned * blocks : (tile_turned + 1) * blocks, :]
                .rearrange("p b c -> p (b c)")
                .bitcast(F32),
            )

        def regroup_v(head, piece, on_scalar=False):
            if piece == 0:
                v_grouped[head] = operands.tile([P, PASSES, D, PACK], BF16, name="v_grouped", bufs=1, align_bytes=64)
            g, part = divmod(piece, V_PIECES // PASSES)
            width = D * PASSES // V_PIECES
            dst = v_grouped[head][:, g, part * width : (part + 1) * width, :]
            src = v_raw[head][:, PACK * g : PACK * (g + 1), part * width : (part + 1) * width].rearrange("p t d -> p d t")
            if on_scalar:
                nc.scalar.copy(out=dst, in_=src)
            else:
                nc.gpsimd.tensor_scalar(out=dst, in0=src, scalar1=1.0, scalar2=0.0, op0=ALU.mult, op1=ALU.add)

        def quantise_v(head, first_part, count):
            if first_part == 0:
                v_words[head] = operands.tile([P, PASSES, D], U32, name="v_words", align_bytes=64)
                v_scales[head] = operands.tile([P, PASSES, D], U8, name="v_scales", align_bytes=64)
            width = PASSES * D // V_PARTS
            words = slice(first_part * width, (first_part + count) * width)
            nc.vector.quantize_mx(
                out=v_words[head][:].rearrange("p g d -> p (g d)")[:, words].bitcast(FP8X4),
                scales=v_scales[head][:].rearrange("p g d -> p (g d)")[:, words],
                in_=v_grouped[head][:].rearrange("p g d t -> p (g d t)")[:, PACK * words.start : PACK * words.stop],
            )

        def scores(j, key_half, chunks=range(4)):
            head, i = divmod(j, TILES)
            if chunks[0] == 0:
                score[(j, key_half)] = score_banks.tile([P, BANK], F32, name="score", tag="score")
            for c in chunks:
                u, member = divmod(c, 2)
                nc.tensor.matmul(
                    score[(j, key_half)][:],
                    lhsT=q_t[head][:, i, u, :].bitcast(BF16).rearrange("p (q e) -> p q e", e=2)[:, :, member],
                    rhs=k_t[head][:, u, key_half * BANK : (key_half + 1) * BANK]
                    .bitcast(BF16)
                    .rearrange("p (n e) -> p n e", e=2)[:, :, member],
                    start=(c == 0),
                    stop=(c == 3),
                )

        def add_bias(j, key_half):
            head, i = divmod(j, TILES)
            h = HEADS[head][1]
            if key_half == 0:
                neg_s[j] = work.tile([P, N + 1], F32, name="neg_s")
            keys = slice(key_half * BANK, (key_half + 1) * BANK)
            nc.vector.scalar_tensor_tensor(
                out=neg_s[j][:, keys].rearrange("q (t p) -> q t p", t=PACK),
                in0=score[(j, key_half)][:].rearrange("q (t p) -> q t p", t=PACK),
                scalar=neg_factor[:, h : h + 1],
                in1=bias_sb[h][:, i, keys].rearrange("q (p t) -> q t p", t=PACK),
                op0=ALU.mult,
                op1=ALU.subtract,
            )

        def row_maximum(j):
            neg_max[j] = columns.tile([P, 1], F32, name="neg_max")
            nc.vector.tensor_reduce(out=neg_max[j][:], in_=neg_s[j][:, :N], axis=AXIS.X, op=ALU.min)

        def of_tile(pairs, j):
            if j // 2 not in pairs:
                pairs[j // 2] = columns.tile([P, 2], F32, name="sums")
            return pairs[j // 2][:, j % 2 : j % 2 + 1]

        def exponential(j):
            e_bf[j] = work.tile([P, N], BF16, name="e_bf")
            nc.scalar.activation(
                out=e_bf[j][:].rearrange("q (b p e) -> q b p e", p=P, e=2),
                in_=neg_s[j][:, :N].rearrange("q (b e p) -> q b p e", p=P, e=2),
                func=ACT.Exp,
                bias=neg_max[j][:],
                scale=-1.0,
                accum_out=of_tile(row_sums, j),
            )

        def transpose_e(j):
            e_bank[j] = transpose_banks.tile([P, 2 * PASSES, P], F32, name="e_bank", tag="bank")
            for block in range(2 * PASSES):
                nc.tensor.transpose(
                    e_bank[j][:, block, :], e_bf[j][:, 2 * block * P : 2 * (block + 1) * P].bitcast(F32), identity_f32[:]
                )

        def regroup_e(j):
            e_grouped[j] = work.tile([P, PASSES, P, PACK], BF16, name="e_grouped", align_bytes=64)
            nc.scalar.copy(
                out=e_grouped[j][:].rearrange("p g q t -> p (g q t)").bitcast(F32).rearrange("p (g q u) -> p g q u", q=P, u=2),
                in_=e_bank[j][:].rearrange("p (g u) q -> p g q u", u=2),
            )

        def quantise_e(j):
            e_words[j] = work.tile([P, PASSES * P], U32, name="e_words", align_bytes=64)
            e_scales[j] = work.tile([P, PASSES * P], U8, name="e_scales", align_bytes=64)
            nc.vector.quantize_mx(
                out=e_words[j][:].bitcast(FP8X4),
                scales=e_scales[j][:],
                in_=e_grouped[j][:].rearrange("p g q t -> p (g q t)"),
            )

        def invert_two_sums(j):
            inv_sums[j // 2] = columns.tile([P, 2], F32, name="inv_sums")
            nc.vector.reciprocal(out=inv_sums[j // 2][:], in_=row_sums[j // 2][:])

        def invert_sum(j):
            nc.vector.reciprocal(out=of_tile(inv_sums, j), in_=of_tile(row_sums, j))

        def mx_passes(j):
            head = j // TILES
            if j < FIRST_LATE_TILE:
                x_bank[j] = output_banks.tile([P, D], F32, name="x_bank", tag="x_bank")
            else:
                x_bank[j] = score_banks.tile([P, D], F32, name="late_x_bank", tag="score")
            for g in range(PASSES):
                queries = slice(g * P, (g + 1) * P)
                nc.tensor.matmul_mx(
                    out=x_bank[j][:],
                    lhsT=e_words[j][:, queries].bitcast(FP8X4),
                    lhsT_scale=e_scales[j][:, queries],
                    rhs=v_words[head][:, g, :].bitcast(FP8X4),
                    rhs_scale=v_scales[head][:, g, :],
                    start=(g == 0),
                    stop=(g == PASSES - 1),
                )

        def normalise(dst, src, inverse, on_vector):
            if on_vector:
                nc.vector.tensor_scalar(out=dst, in0=src, scalar1=inverse, scalar2=None, op0=ALU.mult)
            else:
                nc.scalar.activation(out=dst, in_=src, func=ACT.Copy, scale=inverse)

        def store(j, x_sb, columns_of_d, queue=nc.sync):
            head, i = divmod(j, TILES)
            b, h = HEADS[head]
            row0 = b * N + i * P
            queue.dma_start(
                out=out_rows[row0 : row0 + P, h : h + 1, columns_of_d], in_=x_sb[:].rearrange("p (o d) -> p o d", o=1)
            )

        def output(j, on_vector=False):
            x_sb = work.tile([P, D], F32, name="x_sb")
            normalise(x_sb[:], x_bank[j][:], of_tile(inv_sums, j), on_vector)
            store(j, x_sb, slice(0, D))

        half_sum, half_e, half_bank, half_grouped, half_words, half_scales, half_x_bank = {}, {}, {}, {}, {}, {}, {}

        def first_half_maximum(j):
            nc.vector.tensor_reduce(out=neg_s[j][:, N : N + 1], in_=neg_s[j][:, :BANK], axis=AXIS.X, op=ALU.min)

        def second_half_maximum(j):
            neg_max[j] = columns.tile([P, 1], F32, name="neg_max")
            nc.vector.tensor_reduce(out=neg_max[j][:], in_=neg_s[j][:, BANK:], axis=AXIS.X, op=ALU.min)

        def half_exponential(j, g):
            if g == 0:
                half_sum[j] = columns.tile([P, PASSES], F32, name="half_sum")
            half_e[g] = work.tile([P, BANK], BF16, name="half_e")
            nc.scalar.activation(
                out=half_e[g][:].rearrange("q (b p e) -> q b p e", p=P, e=2),
                in_=neg_s[j][:, g * BANK : (g + 1) * BANK].rearrange("q (b e p) -> q b p e", p=P, e=2),
                func=ACT.Exp,
                bias=neg_max[j][:],
                scale=-1.0,
                accum_out=half_sum[j][:, g : g + 1],
            )

        def half_transpose(g):
            half_bank[g] = transpose_banks.tile([P, 2, P], F32, name="half_bank", tag="bank")
            for u in range(2):
                nc.tensor.transpose(
                    half_bank[g][:, u, :], half_e[g][:, 2 * u * P : 2 * (u + 1) * P].bitcast(F32), identity_f32[:]
                )

        def half_regroup(g):
            half_grouped[g] = work.tile([P, P * PACK], BF16, name="half_grouped", align_bytes=64)
            nc.scalar.copy(
                out=half_grouped[g][:].bitcast(F32).rearrange("p (q u) -> p q u", u=2),
                in_=half_bank[g][:].rearrange("p u q -> p q u"),
            )

        def half_quantise(g):
            half_words[g] = work.tile([P, P], U32, name="half_words", align_bytes=64)
            half_scales[g] = work.tile([P, P], U8, name="half_scales", align_bytes=64)
            nc.vector.quantize_mx(out=half_words[g][:].bitcast(FP8X4), scales=half_scales[g][:], in_=half_grouped[g][:])

        def join_sum(j):
            nc.vector.tensor_reduce(out=of_tile(row_sums, j), in_=half_sum[j][:], axis=AXIS.X, op=ALU.add)

        def mx_pass_by_halves(j, g, words, scales):
            head = j // TILES
            for half in range(2):
                if g == 0:
                    half_x_bank[(j, half)] = score_banks.tile([P, D], F32, name="half_x_bank", tag="score")
                part = slice(half * D // 2, (half + 1) * D // 2)
                nc.tensor.matmul_mx(
                    out=half_x_bank[(j, half)][:, : D // 2],
                    lhsT=words.bitcast(FP8X4),
                    lhsT_scale=scales,
                    rhs=v_words[head][:, g, part].bitcast(FP8X4),
                    rhs_scale=v_scales[head][:, g, part],
                    start=(g == 0),
                    stop=(g == PASSES - 1),
                )

        def output_by_halves(j):
            for half, queue in enumerate((nc.sync, nc.scalar)):
                x_sb = work.tile([P, D // 2], F32, name="half_x_sb")
                normalise(x_sb[:], half_x_bank[(j, half)][:, : D // 2], of_tile(inv_sums, j), on_vector=(half == 0))
                store(j, x_sb, slice(half * D // 2, (half + 1) * D // 2), queue)

        zeros = const.tile([P, BANK], BF16, name="zeros")
        nc.vector.memset(zeros[:], 0.0)

        def warm_up(count):
            bank = score_banks.tile([P, BANK], F32, name="warm_bank", tag="score")
            for repeat in range(count):
                nc.tensor.matmul(bank[:], lhsT=zeros[:, :P], rhs=zeros[:], start=True, stop=True)

        identity_f32 = const.tile([P, P], F32, name="identity_f32")
        make_identity(nc, identity_f32[:])
        bias_sb = [const.tile([P, TILES, N], BF16, name="bias%d" % h) for h in range(NHEADS)]
        new_raw(0)
        new_operands(0)
        load_first_keys(k_raw[0], k_rows, first_row(0), 0, 2)
        load_blocks(q_raw[0], q_rows, first_row(0), 0, 1)
        load_first_keys(k_raw[0], k_rows, first_row(0), 2, 2)
        load_keys(k_raw[0], k_rows, first_row(0), 4, 4)
        log_factor = const.tile([P, NHEADS], BF16, name="log_factor")
        nc.sync.dma_start(out=log_factor[:], in_=logit_scale.rearrange("h a b -> (h a b)").partition_broadcast(P))
        load_blocks(bias_sb[0], bias_rows, 0, 0, 1)
        load_blocks(q_raw[0], q_rows, first_row(0), 1, 3)
        load_keys(v_raw[0], v_rows, first_row(0), 0, TILES)
        load_blocks(bias_sb[0], bias_rows, 0, 1, 1)
        load_blocks(q_raw[0], q_rows, first_row(0), 4, 4)
        load_blocks(bias_sb[0], bias_rows, 0, 2, 2)
        new_raw(1)
        load_keys(k_raw[1], k_rows, first_row(1), 0, TILES)
        load_blocks(bias_sb[0], bias_rows, 0, 4, 2)

        unread = const.tile([P, 1], F32, name="unread")
        nc.scalar.activation(out=unread[:], in_=zeros[:, :1], func=ACT.Exp)

        warm_up(WARM_UP)
        for members in (range(2), range(2, 4)):
            for unit in range(2):
                unit_transposes(0, unit, members)
                unit_copy(0, unit, on_vector=(unit == 1), members=members)
            if members[0] == 0:
                unit_transposes(0, 4, members, in_output_bank=True)
                unit_copy(0, 4, on_vector=True, members=members)
        warm_up(WARM_UP_AGAIN)

        factor = const.tile([P, NHEADS], F32, name="factor")
        nc.scalar.activation(out=factor[:], in_=log_factor[:], func=ACT.Exp)
        neg_factor = const.tile([P, NHEADS], F32, name="neg_factor")
        nc.vector.tensor_scalar(
            out=neg_factor[:], in0=factor[:], scalar1=100.0, scalar2=-1.0, op0=ALU.min, op1=ALU.mult
        )

        scores(0, 0, chunks=range(2))
        unit_transposes(0, 2, in_output_bank=True)
        unit_copy(0, 2, on_vector=False)
        unit_transposes(0, 3)
        unit_copy(0, 3, on_vector=True)
        scores(0, 0, chunks=range(2, 4))
        unit_transposes(0, 4, members=range(2, 4))
        unit_copy(0, 4, on_vector=False, members=range(2, 4))

        for piece in range(V_PIECES - SCALAR_PIECES):
            regroup_v(0, piece)

        def is_tile(j):
            return 0 <= j < ALL_TILES

        for step in range(ALL_TILES):
            head, i = divmod(step, TILES)
            prepare = head + 1
            preparing = prepare < len(HEADS)

            for loaded in range(1, len(HEADS)):
                if step == LOAD_STEP[loaded]:
                    new_raw(loaded)
                    load_keys(k_raw[loaded], k_rows, first_row(loaded), 0, TILES)
                if step == LOAD_STEP[loaded] + 1:
                    load_blocks(q_raw[loaded], q_rows, first_row(loaded), 0, TURNED_FROM[loaded])
                    load_queries_to_turn(loaded)
                if step == LOAD_STEP[loaded] + 2:
                    load_keys(v_raw[loaded], v_rows, first_row(loaded), 0, TILES)
            if step == 2:
                load_blocks(bias_sb[0], bias_rows, 0, 6, 2)
            if step in (3, 4):
                load_blocks(bias_sb[1], bias_rows, N, 4 * (step - 3), 4)

            if preparing and i == 0:
                new_operands(prepare)
            units = []
            if i in OWN_UNIT_STEPS and 2 * OWN_UNIT_STEPS.index(i) + 2 < TURNED_FROM[head]:
                units.append((head, 5 + OWN_UNIT_STEPS.index(i)))
            if preparing:
                units.extend((prepare, unit) for unit, unit_step in enumerate(UNIT_STEPS[prepare]) if unit_step == i)

            if step > 0:
                scores(step, 0)
            if step > MX_LAG:
                mx_passes(step - MX_LAG)
            scores(step, 1)
            if step == MX_LAG:
                mx_passes(0)
            if is_tile(step - TRANSPOSE_LAG):
                transpose_e(step - TRANSPOSE_LAG)
            for count, (unit_head, unit) in enumerate(units):
                unit_transposes(unit_head, unit, in_output_bank=(count > 0))

            add_bias(step, 0)
            if is_tile(step - QUANTISE_LAG):
                quantise_e(step - QUANTISE_LAG)
            v_head, part = divmod(step + TILES - V_FIRST_STEP - 1, TILES)
            if 0 < v_head < len(HEADS) and part < V_PARTS:
                quantise_v(v_head, part, 1)
            if step == LAST:
                first_half_maximum(step)
            add_bias(step, 1)
            if preparing:
                first_turn = (i - FIRST_TURN_STEP[prepare]) * TURNS_A_STEP
                turns = 2 * (TILES - TURNED_FROM[prepare])
                for turn in range(max(first_turn, 0), min(first_turn + TURNS_A_STEP, turns)):
                    turn_queries(prepare, turn)
            if is_tile(step - QUANTISE_LAG) and (step - QUANTISE_LAG) % 2 == 0:
                invert_two_sums(step - QUANTISE_LAG)
            if step == LAST:
                second_half_maximum(step)
            else:
                row_maximum(step)
            if step == MX_LAG - 2:
                quantise_v(0, 0, V_PARTS)

            if is_tile(step - EXP_LAG):
                exponential(step - EXP_LAG)
            if is_tile(step - MX_LAG):
                output(step - MX_LAG)
            if is_tile(step - TRANSPOSE_LAG):
                regroup_e(step - TRANSPOSE_LAG)
            for unit_head, unit in units:
                unit_copy(unit_head, unit, on_vector=False)
            if step < SCALAR_PIECES:
                regroup_v(0, V_PIECES - 1 - step, on_scalar=True)

            v_head, part = divmod(step + TILES - V_FIRST_STEP, TILES)
            if 0 < v_head < len(HEADS) and part < V_PARTS:
                unread_word = columns.tile([P, 1], U32, name="unread_word")
                nc.gpsimd.tensor_copy(out=unread_word[:], in_=e_words[step - QUANTISE_LAG][:, :1])
                for piece in range(part * V_PIECES_A_PART, (part + 1) * V_PIECES_A_PART):
                    regroup_v(v_head, piece)

        mx_passes(LAST - 3)
        transpose_e(LAST - 1)
        regroup_e(LAST - 1)
        half_exponential(LAST, 0)
        half_exponential(LAST, 1)
        quantise_e(LAST - 2)
        mx_passes(LAST - 2)
        quantise_e(LAST - 1)
        invert_sum(LAST - 1)
        output(LAST - 3, on_vector=True)
        half_transpose(0)
        half_transpose(1)
        for g in range(PASSES):
            queries = slice(g * P, (g + 1) * P)
            mx_pass_by_halves(LAST - 1, g, e_words[LAST - 1][:, queries], e_scales[LAST - 1][:, queries])
        join_sum(LAST)
        output(LAST - 2, on_vector=True)
        half_regroup(0)
        half_quantise(0)
        half_regroup(1)
        half_quantise(1)
        for g in range(PASSES):
            mx_pass_by_halves(LAST, g, half_words[g][:], half_scales[g][:])
        invert_sum(LAST)
        output_by_halves(LAST - 1)
        output_by_halves(LAST)
